import numpy as np
import ml_dtypes


def mxq(x, axis, fmt="e4m3"):
    dtype, down = {"e4m3": (ml_dtypes.float8_e4m3fn, 7), "e5m2": (ml_dtypes.float8_e5m2, 14)}[fmt]
    v = np.moveaxis(np.asarray(x, np.float32).astype(ml_dtypes.bfloat16).astype(np.float64), axis, -1)
    blocks = v.reshape(v.shape[:-1] + (-1, 32))
    amax = np.abs(blocks).max(-1, keepdims=True)
    byte = np.maximum(np.where(amax > 0, np.frexp(amax)[1] - 1 + 127, 0) - down, 1)
    scale = np.exp2(byte - 127.0)
    codes = (blocks / scale).astype(np.float32).astype(dtype).astype(np.float64)
    return np.moveaxis((codes * scale).reshape(v.shape), -1, axis)


WIDE = False


def mx_kscale(k):
    if not WIDE:
        return np.ones(k)
    levels = np.array([10, -10, 5, -5, 0])
    a = np.random.permutation(np.resize(levels, k // 512 * 4)).reshape(k // 512, 4)
    idx = np.arange(k)
    return np.exp2(a[idx // 512, idx % 128 // 32])


BF16 = ml_dtypes.bfloat16


def bf(x):
    return np.asarray(x, np.float32).astype(BF16)


def f64(x):
    return np.asarray(x).astype(np.float64)


E2M1 = np.array([0.0, 0.5, 1.0, 1.5, 2.0, 3.0, 4.0, 6.0, -0.0, -0.5, -1.0, -1.5, -2.0, -3.0, -4.0, -6.0])


def pack_weight(w, fmt):
    k, n = w.shape
    w = f64(bf(w)).reshape(k // 32, 32, n)
    amax = np.abs(w).max(1)
    if fmt == "e4m3":
        byte = np.frexp(amax)[1] - 1 + 127 - 7
    else:
        mant, ex = np.frexp(amax / 6.0)
        byte = np.where(mant > 0.5, ex, ex - 1) + 127
    byte = np.clip(np.where(amax > 0, byte, 1), 1, 254)
    scaled = (w * np.exp2(127.0 - byte)[:, None, :]).reshape(k, n).astype(np.float32)
    by_word = np.ascontiguousarray(scaled.reshape(k // 512, 128, 4, n).transpose(0, 1, 3, 2))
    if fmt == "e4m3":
        words = by_word.astype(ml_dtypes.float8_e4m3fn).view(np.uint8)
    else:
        c = by_word.astype(ml_dtypes.float4_e2m1fn).view(np.uint8) & 0xF
        words = c[..., 0::2] | (c[..., 1::2] << 4)
    return np.ascontiguousarray(words), np.ascontiguousarray(byte.astype(np.uint8).reshape(k // 512, 16, n))


def unpack_weight(words, scales, fmt):
    g, p, n, _ = words.shape
    if fmt == "e4m3":
        vals = np.ascontiguousarray(words).view(ml_dtypes.float8_e4m3fn).astype(np.float64)
    else:
        nib = np.empty((g, p, n, 4), np.uint8)
        nib[..., 0::2] = words & 0xF
        nib[..., 1::2] = words >> 4
        vals = E2M1[nib]
    vals = vals * np.repeat(np.exp2(scales.astype(np.float64) - 127.0), 8, axis=1)[..., None]
    return vals.transpose(0, 1, 3, 2).reshape(g * 512, n)


B, N, H, DH, E, W, DQ, DKV = 8, 512, 4, 128, 2, 128, 1024, 512
DV = E * DH
DM = H * DV
NEG = -3.4028234663852886e38


def silu(v):
    return v / (1.0 + np.exp(-v))


def split_heads(t):
    return t.reshape(B, N, H, DV).transpose(0, 2, 1, 3)


def setup_inputs():
    s = mx_kscale(DKV)
    q = bf(np.random.standard_normal((B, H, N, DH)) * 1.4)
    k1 = bf(np.random.standard_normal((B, H, N, DH)) * 1.4)
    key_values_input = bf(np.random.standard_normal((B, N, DKV)) * s)
    words, scales = pack_weight(np.random.standard_normal((DKV, DM)) * 4.0 / np.sqrt(DKV) / s[:, None], "e4m3")
    attn_sink = bf(np.log(N) + 0.5 + 0.5 * np.random.standard_normal(H))
    return {"q": q,
            "k1": k1,
            "key_values_input": key_values_input,
            "Wv1_words": words,
            "Wv1_scales": scales,
            "attn_sink": attn_sink}


def reference(q, k1, key_values_input, Wv1_words, Wv1_scales, attn_sink):
    v1 = split_heads(mxq(f64(key_values_input), 2, "e4m3") @ unpack_weight(Wv1_words, Wv1_scales, "e4m3"))
    sim = f64(q) @ f64(k1).transpose(0, 1, 3, 2) * DH ** -0.5
    idx = np.arange(N)
    mask = (idx[None, :] > idx[:, None]) & (idx[None, :] - idx[:, None] <= W)
    sim = np.where(mask, NEG, sim)
    sink = f64(attn_sink)[None, :, None, None]
    m = np.maximum(sim.max(-1, keepdims=True), sink)
    e = np.exp(sim - m)
    den = e.sum(-1, keepdims=True) + np.exp(sink - m)
    return silu((mxq(e, 3, "e4m3") @ mxq(v1, 2, "e4m3")) / den)

@@ -1,0 +1,373 @@
+from contextlib import ExitStack
+
+import concourse.mybir as mybir
+from concourse.masks import make_identity
+
+F32 = mybir.dt.float32
+BF16 = mybir.dt.bfloat16
+I32 = mybir.dt.int32
+U32 = mybir.dt.uint32
+U8 = mybir.dt.uint8
+FP8X4 = mybir.dt.float8_e4m3fn_x4
+ALU = mybir.AluOpType
+FUNC = mybir.ActivationFunctionType
+AXIS = mybir.AxisListType
+
+B, H, N, DH, DV, DKV = 8, 4, 512, 128, 256, 512
+DM = H * DV
+P = 128
+NT = N // P
+PACK = 4
+SCALE = DH ** -0.5
+FLT_MAX = 3.4028234663852886e38
+
+UNITS = B * H
+
+FLOPS = 2 * B * N * DKV * DM + 2 * B * H * N * N * DH + 2 * B * H * N * N * DV
+
+
+def blocks_outside_window(i_tile):
+    free = [a for a in range(NT) if a not in (i_tile, i_tile + 1)]
+    return slice(free[0], free[-1] + 1, free[1] - free[0])
+
+
+def tile_attention_pa_t_kernel(tc, q, k1, key_values_input, Wv1_words, Wv1_scales, attn_sink, out):
+    nc = tc.nc
+    with ExitStack() as stack:
+        const = stack.enter_context(tc.tile_pool(name="const", bufs=1))
+        loads = stack.enter_context(tc.tile_pool(name="loads", bufs=3))
+        values = stack.enter_context(tc.tile_pool(name="values", bufs=2))
+        work = stack.enter_context(tc.tile_pool(name="work", bufs=2))
+        results = stack.enter_context(tc.tile_pool(name="results", bufs=3))
+        small = stack.enter_context(tc.tile_pool(name="small", bufs=4))
+        logit_banks = stack.enter_context(tc.psum_pool(name="logit_banks", bufs=4))
+        scratch = stack.enter_context(tc.psum_pool(name="scratch", bufs=2))
+        sums = stack.enter_context(tc.psum_pool(name="sums", bufs=2))
+        stack.enter_context(tc.manual_schedule())
+
+        w_codes = const.tile([P, DM], U32, align_bytes=64)
+        w_scales = const.tile([P, DM], U8, align_bytes=64)
+        nc.vector.memset(w_scales[:].bitcast(I32), 0)
+        for quad in range(4):
+            nc.sync.dma_start(
+                out=w_scales[32 * quad : 32 * quad + 4, :].bitcast(I32),
+                in_=Wv1_scales[0, 4 * quad : 4 * quad + 4, :].bitcast(I32),
+            )
+        sink_bf = const.tile([P, H], BF16)
+        nc.sync.dma_start(out=sink_bf[:], in_=attn_sink.partition_broadcast(P))
+
+        ident_f32 = const.tile([P, P], F32)
+        make_identity(nc, ident_f32[:])
+        ident_bf = const.tile([P, P], BF16)
+        make_identity(nc, ident_bf[:])
+
+        cap = const.tile([P, 2, P], F32)
+        nc.gpsimd.memset(cap[:], FLT_MAX)
+        nc.gpsimd.affine_select(
+            out=cap[:, 0, :], in_=cap[:, 0, :], pattern=[[-1, P]], compare_op=ALU.is_ge,
+            fill=-FLT_MAX, base=0, channel_multiplier=1,
+        )
+        nc.gpsimd.affine_select(
+            out=cap[:, 1, :], in_=cap[:, 1, :], pattern=[[1, P]], compare_op=ALU.is_ge,
+            fill=-FLT_MAX, base=-1, channel_multiplier=-1,
+        )
+        cap_flat = cap[:].rearrange("p a j -> p (a j)")
+
+        sink = const.tile([P, H], F32)
+        nc.vector.tensor_copy(out=sink[:], in_=sink_bf[:])
+        neg_sink = const.tile([P, H], F32)
+        nc.vector.tensor_scalar(out=neg_sink[:], in0=sink[:], scalar1=-1.0, scalar2=None, op0=ALU.mult)
+
+        kept = {}
+
+        def load_sequence(b):
+            kv_sb = loads.tile([P, NT, DKV], BF16)
+            nc.sync.dma_start(
+                out=kv_sb[:].rearrange("p (u e) k -> p u (e k)", e=2),
+                in_=key_values_input[b].rearrange("(u p e) k -> p u (e k)", u=2, e=2),
+            )
+            q_sb = loads.tile([P, H * NT, DH], BF16)
+            nc.sync.dma_start(out=q_sb[:], in_=q[b].rearrange("h (t p) d -> p (h t) d", p=P))
+            k_sb = loads.tile([P, H * NT, DH], BF16)
+            nc.sync.dma_start(out=k_sb[:], in_=k1[b].rearrange("h (t p) d -> p (h t) d", p=P))
+            kept[b, "kv_sb"], kept[b, "q_sb"], kept[b, "k_sb"] = kv_sb, q_sb, k_sb
+
+        def transpose_features(b, half):
+            kv_words = kept[b, "kv_sb"][:].bitcast(F32)
+            kvT_ps = scratch.tile([P, 2, 2, P], F32, tag="scratch")
+            for t2 in range(2):
+                for u in range(2):
+                    nc.tensor.transpose(
+                        kvT_ps[:, t2, u, :], kv_words[:, 2 * half + t2, u : DKV // 2 : 2], ident_f32[:]
+                    )
+            kept[b, "kvT_ps", half] = kvT_ps
+
+        def group_features(b, half):
+            if half == 0:
+                kv_grouped = values.tile([P, N * PACK], BF16, align_bytes=64)
+                kept[b, "kv_grouped"] = kv_grouped
+            kv_grouped_words = kept[b, "kv_grouped"][:].bitcast(F32).rearrange("p (t j u) -> p t j u", t=NT, u=2)
+            nc.vector.tensor_copy(
+                out=kv_grouped_words[:, 2 * half : 2 * half + 2],
+                in_=kept[b, "kvT_ps", half][:].rearrange("p t u j -> p t j u"),
+            )
+
+        def quantise_features(b):
+            kv_codes = values.tile([P, N], U32, align_bytes=64)
+            kv_scales = values.tile([P, N], U8, align_bytes=64)
+            nc.vector.quantize_mx(
+                out=kv_codes[:].bitcast(FP8X4), scales=kv_scales[:], in_=kept[b, "kv_grouped"][:]
+            )
+            v_grouped = values.tile([P, DM * PACK], BF16, align_bytes=64)
+            v_codes = values.tile([P, DM], U32, align_bytes=64)
+            v_scales = values.tile([P, DM], U8, align_bytes=64)
+            kept[b, "kv_codes"], kept[b, "kv_scales"] = kv_codes, kv_scales
+            kept[b, "v_grouped"], kept[b, "v_codes"], kept[b, "v_scales"] = v_grouped, v_codes, v_scales
+
+        def project(unit, piece):
+            b, h = divmod(unit, H)
+            cols = slice((2 * h + piece) * P, (2 * h + piece + 1) * P)
+            v_ps = scratch.tile([P, NT, P], F32, tag="scratch")
+            for t in range(NT):
+                rows = slice(t * P, (t + 1) * P)
+                nc.tensor.matmul_mx(
+                    out=v_ps[:, t, :],
+                    lhsT=kept[b, "kv_codes"][:, rows].bitcast(FP8X4),
+                    lhsT_scale=kept[b, "kv_scales"][:, rows],
+                    rhs=w_codes[:, cols].bitcast(FP8X4),
+                    rhs_scale=w_scales[:, cols],
+                    start=True,
+                    stop=True,
+                )
+            kept[unit, "v_ps", piece] = v_ps
+
+        def round_values(unit, piece):
+            b, h = divmod(unit, H)
+            first = (2 * h + piece) * P * PACK
+            grouped = kept[b, "v_grouped"][:, first : first + P * PACK].rearrange("p (n t) -> p n t", t=PACK)
+            by_column = kept[unit, "v_ps", piece][:].rearrange("p t n -> p n t")
+            if piece == 0:
+                nc.vector.tensor_copy(out=grouped, in_=by_column)
+            else:
+                nc.scalar.copy(out=grouped, in_=by_column)
+
+        def quantise_values(unit):
+            b, h = divmod(unit, H)
+            head = slice(h * DV, (h + 1) * DV)
+            nc.vector.quantize_mx(
+                out=kept[b, "v_codes"][:, head].bitcast(FP8X4),
+                scales=kept[b, "v_scales"][:, head],
+                in_=kept[b, "v_grouped"][:, h * DV * PACK : (h + 1) * DV * PACK],
+            )
+
+        def transpose_qk(unit):
+            b, h = divmod(unit, H)
+            qkT_ps = scratch.tile([P, 2 * NT, P], BF16, tag="scratch")
+            for t in range(NT):
+                nc.tensor.transpose(qkT_ps[:, t, :], kept[b, "q_sb"][:, h * NT + t, :], ident_bf[:])
+            for t in range(NT):
+                nc.tensor.transpose(qkT_ps[:, NT + t, :], kept[b, "k_sb"][:, h * NT + t, :], ident_bf[:])
+            kept[unit, "qkT_ps"] = qkT_ps
+
+        def copy_qk(unit):
+            qkT = work.tile([P, 2 * N], BF16)
+            nc.scalar.copy(out=qkT[:], in_=kept[unit, "qkT_ps"][:].rearrange("p t i -> p (t i)"))
+            kept[unit, "qkT"] = qkT
+
+        def logits(unit):
+            qkT = kept[unit, "qkT"]
+            for it in range(NT):
+                s_ps = logit_banks.tile([P, NT, P], F32)
+                nc.tensor.matmul(
+                    out=s_ps[:].rearrange("p a j -> p (a j)"),
+                    lhsT=qkT[:, it * P : (it + 1) * P],
+                    rhs=qkT[:, N : 2 * N],
+                    start=True,
+                    stop=True,
+                )
+                kept[unit, "s_ps", it] = s_ps
+            masked = work.tile([P, NT, 2 * P], F32)
+            row_max = small.tile([P, NT, 2], F32)
+            kept[unit, "masked"], kept[unit, "row_max"] = masked, row_max
+
+        def mask_and_max(unit, it):
+            s_ps, masked, row_max = kept[unit, "s_ps", it], kept[unit, "masked"], kept[unit, "row_max"]
+            width = min(2 * P, N - it * P)
+            nc.vector.tensor_tensor(
+                out=masked[:, it, :width],
+                in0=s_ps[:].rearrange("p a j -> p (a j)")[:, it * P : it * P + width],
+                in1=cap_flat[:, :width],
+                op=ALU.min,
+            )
+            nc.vector.tensor_reduce(
+                out=row_max[:, it, 1:2], in_=s_ps[:, blocks_outside_window(it), :], axis=AXIS.XY, op=ALU.max
+            )
+            nc.vector.tensor_reduce(out=row_max[:, it, 0:1], in_=masked[:, it, :width], axis=AXIS.X, op=ALU.max)
+
+        def finish_max(unit):
+            h = unit % H
+            s_max = small.tile([P, NT], F32)
+            nc.vector.tensor_reduce(out=s_max[:], in_=kept[unit, "row_max"][:], axis=AXIS.X, op=ALU.max)
+            neg_m = small.tile([P, NT], F32)
+            nc.vector.tensor_scalar(
+                out=neg_m[:], in0=s_max[:], scalar1=-SCALE, scalar2=neg_sink[:, h : h + 1],
+                op0=ALU.mult, op1=ALU.min,
+            )
+            kept[unit, "neg_m"] = neg_m
+
+        def exp_outside(unit):
+            neg_m = kept[unit, "neg_m"]
+            e_sb = work.tile([P, NT, N], BF16)
+            den_parts = small.tile([P, NT, 3], F32)
+            kept[unit, "e_sb"], kept[unit, "den_parts"] = e_sb, den_parts
+            for it in range(NT):
+                outside = blocks_outside_window(it)
+                nc.scalar.activation(
+                    out=e_sb[:, it, :].rearrange("p (a j) -> p a j", j=P)[:, outside, :],
+                    in_=kept[unit, "s_ps", it][:, outside, :], func=FUNC.Exp,
+                    bias=neg_m[:, it : it + 1], scale=SCALE, accum_out=den_parts[:, it, 1:2],
+                )
+
+        def exp_window(unit, half):
+            h = unit % H
+            neg_m, e_sb, den_parts = kept[unit, "neg_m"], kept[unit, "e_sb"], kept[unit, "den_parts"]
+            for it in range(2 * half, 2 * half + 2):
+                width = min(2 * P, N - it * P)
+                nc.scalar.activation(
+                    out=e_sb[:, it, it * P : it * P + width], in_=kept[unit, "masked"][:, it, :width],
+                    func=FUNC.Exp, bias=neg_m[:, it : it + 1], scale=SCALE, accum_out=den_parts[:, it, 0:1],
+                )
+            if half == 1:
+                nc.scalar.activation(
+                    out=den_parts[:, :, 2], in_=neg_m[:], func=FUNC.Exp, bias=sink[:, h : h + 1], scale=1.0
+                )
+
+        def denominators(unit):
+            den = small.tile([P, NT], F32)
+            nc.vector.tensor_reduce(out=den[:], in_=kept[unit, "den_parts"][:], axis=AXIS.X, op=ALU.add)
+            inv_den = small.tile([P, NT], F32)
+            nc.vector.reciprocal(out=inv_den[:], in_=den[:])
+            half_inv_den = small.tile([P, NT], F32)
+            nc.vector.tensor_scalar(out=half_inv_den[:], in0=inv_den[:], scalar1=0.5, scalar2=None, op0=ALU.mult)
+            kept[unit, "half_inv_den"] = half_inv_den
+
+        def transpose_e(unit, half):
+            e_words = kept[unit, "e_sb"][:].bitcast(F32)
+            eT_ps = scratch.tile([P, 2, 2, P], F32, tag="scratch")
+            for t2 in range(2):
+                for u in range(2):
+                    nc.tensor.transpose(
+                        eT_ps[:, t2, u, :], e_words[:, 2 * half + t2, u * P : (u + 1) * P], ident_f32[:]
+                    )
+            kept[unit, "eT_ps", half] = eT_ps
+
+        def group_e(unit, half):
+            if half == 0:
+                e_grouped = work.tile([P, N * PACK], BF16, align_bytes=64)
+                kept[unit, "e_grouped"] = e_grouped
+            e_grouped_words = kept[unit, "e_grouped"][:].bitcast(F32).rearrange("p (t i u) -> p t i u", t=NT, u=2)
+            nc.scalar.copy(
+                out=e_grouped_words[:, 2 * half : 2 * half + 2],
+                in_=kept[unit, "eT_ps", half][:].rearrange("p t u i -> p t i u"),
+            )
+
+        def quantise_e(unit):
+            e_codes = work.tile([P, N], U32, align_bytes=64)
+            e_scales = work.tile([P, N], U8, align_bytes=64)
+            nc.vector.quantize_mx(
+                out=e_codes[:].bitcast(FP8X4), scales=e_scales[:], in_=kept[unit, "e_grouped"][:]
+            )
+            kept[unit, "e_codes"], kept[unit, "e_scales"] = e_codes, e_scales
+
+        def weighted_values(unit):
+            b, h = divmod(unit, H)
+            head = slice(h * DV, (h + 1) * DV)
+            for half in range(2):
+                acc = sums.tile([P, 2, DV], F32)
+                for t2 in range(2):
+                    rows = slice((2 * half + t2) * P, (2 * half + t2 + 1) * P)
+                    nc.tensor.matmul_mx(
+                        out=acc[:, t2, :],
+                        lhsT=kept[unit, "e_codes"][:, rows].bitcast(FP8X4),
+                        lhsT_scale=kept[unit, "e_scales"][:, rows],
+                        rhs=kept[b, "v_codes"][:, head].bitcast(FP8X4),
+                        rhs_scale=kept[b, "v_scales"][:, head],
+                        start=True,
+                        stop=True,
+                    )
+                kept[unit, "acc", half] = acc
+            tanh_sb = results.tile([P, NT, DV], F32)
+            gate = results.tile([P, NT, DV], F32)
+            o_sb = results.tile([P, NT, DV], F32)
+            kept[unit, "tanh_sb"], kept[unit, "gate"], kept[unit, "o_sb"] = tanh_sb, gate, o_sb
+
+        def tanh_gate(unit, half):
+            half_inv_den = kept[unit, "half_inv_den"]
+            for t2 in range(2):
+                it = 2 * half + t2
+                nc.scalar.activation(
+                    out=kept[unit, "tanh_sb"][:, it, :], in_=kept[unit, "acc", half][:, t2, :], func=FUNC.Tanh,
+                    scale=half_inv_den[:, it : it + 1],
+                )
+                nc.gpsimd.tensor_scalar(
+                    out=kept[unit, "gate"][:, it, :], in0=kept[unit, "tanh_sb"][:, it, :], scalar1=1.0,
+                    scalar2=half_inv_den[:, it : it + 1], op0=ALU.add, op1=ALU.mult,
+                )
+
+        def finish(unit, half):
+            pair = slice(2 * half, 2 * half + 2)
+            nc.vector.tensor_tensor(
+                out=kept[unit, "o_sb"][:, pair, :], in0=kept[unit, "acc", half][:],
+                in1=kept[unit, "gate"][:, pair, :], op=ALU.mult,
+            )
+
+        def store(unit):
+            b, h = divmod(unit, H)
+            nc.sync.dma_start(out=out[b, h].rearrange("(t p) c -> p t c", p=P), in_=kept[unit, "o_sb"][:])
+
+        def when_live(stage, unit, *args):
+            if 0 <= unit < UNITS:
+                stage(unit, *args)
+
+        def when_first_head(stage, unit, *args):
+            if 0 <= unit < UNITS and unit % H == 0:
+                stage(unit // H, *args)
+
+        load_sequence(0)
+        nc.sync.dma_start(
+            out=w_codes[:].bitcast(I32), in_=Wv1_words[0].rearrange("p n t -> p (n t)").bitcast(I32)
+        )
+        for n in range(-4, UNITS + 2):
+            if n % H == 0 and n // H + 2 < B:
+                load_sequence(n // H + 2)
+            when_live(finish, n - 2, 0)
+            when_live(finish, n - 2, 1)
+            when_live(store, n - 2)
+            when_live(exp_outside, n)
+            when_live(logits, n + 1)
+            when_live(weighted_values, n - 1)
+            when_live(round_values, n + 1, 0)
+            when_live(exp_window, n, 0)
+            when_live(transpose_e, n, 0)
+            when_live(round_values, n + 1, 1)
+            when_live(exp_window, n, 1)
+            when_live(transpose_e, n, 1)
+            for it in range(NT):
+                when_live(mask_and_max, n + 1, it)
+            when_live(finish_max, n + 1)
+            when_live(tanh_gate, n - 1, 0)
+            when_live(group_e, n, 0)
+            when_live(transpose_qk, n + 2)
+            when_live(tanh_gate, n - 1, 1)
+            when_live(group_e, n, 1)
+            when_live(project, n + 2, 0)
+            when_live(denominators, n)
+            when_live(quantise_values, n + 1)
+            when_live(quantise_e, n)
+            when_live(copy_qk, n + 2)
+            when_first_head(transpose_features, n + 4, 0)
+            when_first_head(transpose_features, n + 3, 1)
+            when_first_head(group_features, n + 4, 0)
+            when_first_head(group_features, n + 3, 1)
+            when_live(project, n + 2, 1)
+            when_first_head(quantise_features, n + 3)

@@ -26,11 +26,6 @@ UNITS = B * H
 FLOPS = 2 * B * N * DKV * DM + 2 * B * H * N * N * DH + 2 * B * H * N * N * DV
 
 
-def blocks_outside_window(i_tile):
-    free = [a for a in range(NT) if a not in (i_tile, i_tile + 1)]
-    return slice(free[0], free[-1] + 1, free[1] - free[0])
-
-
 def tile_attention_pa_t_kernel(tc, q, k1, key_values_input, Wv1_words, Wv1_scales, attn_sink, out):
     nc = tc.nc
     with ExitStack() as stack:
@@ -43,7 +38,6 @@ def tile_attention_pa_t_kernel(tc, q, k1, key_values_input, Wv1_words, Wv1_scale
         logit_banks = stack.enter_context(tc.psum_pool(name="logit_banks", bufs=4))
         scratch = stack.enter_context(tc.psum_pool(name="scratch", bufs=2))
         sums = stack.enter_context(tc.psum_pool(name="sums", bufs=2))
-        stack.enter_context(tc.manual_schedule())
 
         w_codes = const.tile([P, DM], U32, align_bytes=64)
         w_scales = const.tile([P, DM], U8, align_bytes=64)
@@ -61,17 +55,16 @@ def tile_attention_pa_t_kernel(tc, q, k1, key_values_input, Wv1_words, Wv1_scale
         ident_bf = const.tile([P, P], BF16)
         make_identity(nc, ident_bf[:])
 
-        cap = const.tile([P, 2, P], F32)
-        nc.gpsimd.memset(cap[:], FLT_MAX)
+        mask_T = const.tile([P, 2, P], F32)
+        nc.gpsimd.memset(mask_T[:], 0.0)
         nc.gpsimd.affine_select(
-            out=cap[:, 0, :], in_=cap[:, 0, :], pattern=[[-1, P]], compare_op=ALU.is_ge,
-            fill=-FLT_MAX, base=0, channel_multiplier=1,
+            out=mask_T[:, 0, :], in_=mask_T[:, 0, :], pattern=[[1, P]], compare_op=ALU.is_ge,
+            fill=-FLT_MAX, base=0, channel_multiplier=-1,
         )
         nc.gpsimd.affine_select(
-            out=cap[:, 1, :], in_=cap[:, 1, :], pattern=[[1, P]], compare_op=ALU.is_ge,
-            fill=-FLT_MAX, base=-1, channel_multiplier=-1,
+            out=mask_T[:, 1, :], in_=mask_T[:, 1, :], pattern=[[-1, P]], compare_op=ALU.is_ge,
+            fill=-FLT_MAX, base=-1, channel_multiplier=1,
         )
-        cap_flat = cap[:].rearrange("p a j -> p (a j)")
 
         sink = const.tile([P, H], F32)
         nc.vector.tensor_copy(out=sink[:], in_=sink_bf[:])
@@ -146,10 +139,7 @@ def tile_attention_pa_t_kernel(tc, q, k1, key_values_input, Wv1_words, Wv1_scale
             first = (2 * h + piece) * P * PACK
             grouped = kept[b, "v_grouped"][:, first : first + P * PACK].rearrange("p (n t) -> p n t", t=PACK)
             by_column = kept[unit, "v_ps", piece][:].rearrange("p t n -> p n t")
-            if piece == 0:
-                nc.vector.tensor_copy(out=grouped, in_=by_column)
-            else:
-                nc.scalar.copy(out=grouped, in_=by_column)
+            nc.scalar.copy(out=grouped, in_=by_column)
 
         def quantise_values(unit):
             b, h = divmod(unit, H)
@@ -171,75 +161,62 @@ def tile_attention_pa_t_kernel(tc, q, k1, key_values_input, Wv1_words, Wv1_scale
 
         def copy_qk(unit):
             qkT = work.tile([P, 2 * N], BF16)
-            nc.scalar.copy(out=qkT[:], in_=kept[unit, "qkT_ps"][:].rearrange("p t i -> p (t i)"))
+            nc.vector.tensor_copy(out=qkT[:], in_=kept[unit, "qkT_ps"][:].rearrange("p t i -> p (t i)"))
             kept[unit, "qkT"] = qkT
 
-        def logits(unit):
+        def logits(unit, half):
             qkT = kept[unit, "qkT"]
-            for it in range(NT):
+            for it in range(2 * half, 2 * half + 2):
                 s_ps = logit_banks.tile([P, NT, P], F32)
                 nc.tensor.matmul(
                     out=s_ps[:].rearrange("p a j -> p (a j)"),
                     lhsT=qkT[:, it * P : (it + 1) * P],
                     rhs=qkT[:, N : 2 * N],
                     start=True,
-                    stop=True,
+                    stop=False,
                 )
+                masked_tiles = min(2, NT - it)
+                for a in range(masked_tiles):
+                    nc.tensor.matmul(
+                        out=s_ps[:, it + a, :], lhsT=mask_T[:, a, :], rhs=ident_f32[:], is_transpose=True,
+                        start=False, stop=(a == masked_tiles - 1),
+                    )
                 kept[unit, "s_ps", it] = s_ps
-            masked = work.tile([P, NT, 2 * P], F32)
-            row_max = small.tile([P, NT, 2], F32)
-            kept[unit, "masked"], kept[unit, "row_max"] = masked, row_max
 
-        def mask_and_max(unit, it):
-            s_ps, masked, row_max = kept[unit, "s_ps", it], kept[unit, "masked"], kept[unit, "row_max"]
-            width = min(2 * P, N - it * P)
-            nc.vector.tensor_tensor(
-                out=masked[:, it, :width],
-                in0=s_ps[:].rearrange("p a j -> p (a j)")[:, it * P : it * P + width],
-                in1=cap_flat[:, :width],
-                op=ALU.min,
-            )
-            nc.vector.tensor_reduce(
-                out=row_max[:, it, 1:2], in_=s_ps[:, blocks_outside_window(it), :], axis=AXIS.XY, op=ALU.max
-            )
-            nc.vector.tensor_reduce(out=row_max[:, it, 0:1], in_=masked[:, it, :width], axis=AXIS.X, op=ALU.max)
+        def maxima(unit, half):
+            if half == 0:
+                s_max = small.tile([P, NT], F32)
+                kept[unit, "s_max"] = s_max
+            for it in range(2 * half, 2 * half + 2):
+                nc.vector.tensor_reduce(
+                    out=kept[unit, "s_max"][:, it : it + 1], in_=kept[unit, "s_ps", it][:], axis=AXIS.XY, op=ALU.max
+                )
 
         def finish_max(unit):
             h = unit % H
-            s_max = small.tile([P, NT], F32)
-            nc.vector.tensor_reduce(out=s_max[:], in_=kept[unit, "row_max"][:], axis=AXIS.X, op=ALU.max)
             neg_m = small.tile([P, NT], F32)
             nc.vector.tensor_scalar(
-                out=neg_m[:], in0=s_max[:], scalar1=-SCALE, scalar2=neg_sink[:, h : h + 1],
+                out=neg_m[:], in0=kept[unit, "s_max"][:], scalar1=-SCALE, scalar2=neg_sink[:, h : h + 1],
                 op0=ALU.mult, op1=ALU.min,
             )
             kept[unit, "neg_m"] = neg_m
 
-        def exp_outside(unit):
-            neg_m = kept[unit, "neg_m"]
-            e_sb = work.tile([P, NT, N], BF16)
-            den_parts = small.tile([P, NT, 3], F32)
-            kept[unit, "e_sb"], kept[unit, "den_parts"] = e_sb, den_parts
-            for it in range(NT):
-                outside = blocks_outside_window(it)
-                nc.scalar.activation(
-                    out=e_sb[:, it, :].rearrange("p (a j) -> p a j", j=P)[:, outside, :],
-                    in_=kept[unit, "s_ps", it][:, outside, :], func=FUNC.Exp,
-                    bias=neg_m[:, it : it + 1], scale=SCALE, accum_out=den_parts[:, it, 1:2],
-                )
-
-        def exp_window(unit, half):
+        def exponentials(unit, half):
             h = unit % H
-            neg_m, e_sb, den_parts = kept[unit, "neg_m"], kept[unit, "e_sb"], kept[unit, "den_parts"]
+            neg_m = kept[unit, "neg_m"]
+            if half == 0:
+                e_sb = work.tile([P, NT, N], BF16)
+                den_parts = small.tile([P, NT, 2], F32)
+                kept[unit, "e_sb"], kept[unit, "den_parts"] = e_sb, den_parts
+            e_sb, den_parts = kept[unit, "e_sb"], kept[unit, "den_parts"]
             for it in range(2 * half, 2 * half + 2):
-                width = min(2 * P, N - it * P)
                 nc.scalar.activation(
-                    out=e_sb[:, it, it * P : it * P + width], in_=kept[unit, "masked"][:, it, :width],
-                    func=FUNC.Exp, bias=neg_m[:, it : it + 1], scale=SCALE, accum_out=den_parts[:, it, 0:1],
+                    out=e_sb[:, it, :], in_=kept[unit, "s_ps", it][:].rearrange("p a j -> p (a j)"), func=FUNC.Exp,
+                    bias=neg_m[:, it : it + 1], scale=SCALE, accum_out=den_parts[:, it, 0:1],
                 )
             if half == 1:
                 nc.scalar.activation(
-                    out=den_parts[:, :, 2], in_=neg_m[:], func=FUNC.Exp, bias=sink[:, h : h + 1], scale=1.0
+                    out=den_parts[:, :, 1], in_=neg_m[:], func=FUNC.Exp, bias=sink[:, h : h + 1], scale=1.0
                 )
 
         def denominators(unit):
@@ -343,17 +320,17 @@ def tile_attention_pa_t_kernel(tc, q, k1, key_values_input, Wv1_words, Wv1_scale
             when_live(finish, n - 2, 0)
             when_live(finish, n - 2, 1)
             when_live(store, n - 2)
-            when_live(exp_outside, n)
-            when_live(logits, n + 1)
-            when_live(weighted_values, n - 1)
+            when_live(exponentials, n, 0)
+            when_live(logits, n + 1, 0)
             when_live(round_values, n + 1, 0)
-            when_live(exp_window, n, 0)
             when_live(transpose_e, n, 0)
+            when_live(exponentials, n, 1)
+            when_live(logits, n + 1, 1)
             when_live(round_values, n + 1, 1)
-            when_live(exp_window, n, 1)
             when_live(transpose_e, n, 1)
-            for it in range(NT):
-                when_live(mask_and_max, n + 1, it)
+            when_live(weighted_values, n - 1)
+            when_live(maxima, n + 1, 0)
+            when_live(maxima, n + 1, 1)
             when_live(finish_max, n + 1)
             when_live(tanh_gate, n - 1, 0)
             when_live(group_e, n, 0)

@@ -22,6 +22,8 @@ SCALE = DH ** -0.5
 FLT_MAX = 3.4028234663852886e38
 
 UNITS = B * H
+QK_AHEAD = 6
+LOGIT_BANKS = 3
 
 FLOPS = 2 * B * N * DKV * DM + 2 * B * H * N * N * DH + 2 * B * H * N * N * DV
 
@@ -31,12 +33,13 @@ def tile_attention_pa_t_kernel(tc, q, k1, key_values_input, Wv1_words, Wv1_scale
     with ExitStack() as stack:
         const = stack.enter_context(tc.tile_pool(name="const", bufs=1))
         loads = stack.enter_context(tc.tile_pool(name="loads", bufs=3))
+        unit_loads = stack.enter_context(tc.tile_pool(name="unit_loads", bufs=QK_AHEAD + 1))
         values = stack.enter_context(tc.tile_pool(name="values", bufs=2))
-        work = stack.enter_context(tc.tile_pool(name="work", bufs=2))
+        work = stack.enter_context(tc.tile_pool(name="work", bufs=3))
         results = stack.enter_context(tc.tile_pool(name="results", bufs=3))
         small = stack.enter_context(tc.tile_pool(name="small", bufs=4))
-        logit_banks = stack.enter_context(tc.psum_pool(name="logit_banks", bufs=4))
-        scratch = stack.enter_context(tc.psum_pool(name="scratch", bufs=2))
+        logit_banks = stack.enter_context(tc.psum_pool(name="logit_banks", bufs=LOGIT_BANKS))
+        scratch = stack.enter_context(tc.psum_pool(name="scratch", bufs=3))
         sums = stack.enter_context(tc.psum_pool(name="sums", bufs=2))
 
         w_codes = const.tile([P, DM], U32, align_bytes=64)
@@ -73,17 +76,21 @@ def tile_attention_pa_t_kernel(tc, q, k1, key_values_input, Wv1_words, Wv1_scale
 
         kept = {}
 
-        def load_sequence(b):
+        def load_features(b):
             kv_sb = loads.tile([P, NT, DKV], BF16)
             nc.sync.dma_start(
                 out=kv_sb[:].rearrange("p (u e) k -> p u (e k)", e=2),
                 in_=key_values_input[b].rearrange("(u p e) k -> p u (e k)", u=2, e=2),
             )
-            q_sb = loads.tile([P, H * NT, DH], BF16)
-            nc.sync.dma_start(out=q_sb[:], in_=q[b].rearrange("h (t p) d -> p (h t) d", p=P))
-            k_sb = loads.tile([P, H * NT, DH], BF16)
-            nc.sync.dma_start(out=k_sb[:], in_=k1[b].rearrange("h (t p) d -> p (h t) d", p=P))
-            kept[b, "kv_sb"], kept[b, "q_sb"], kept[b, "k_sb"] = kv_sb, q_sb, k_sb
+            kept[b, "kv_sb"] = kv_sb
+
+        def load_qk(unit):
+            b, h = divmod(unit, H)
+            q_sb = unit_loads.tile([P, NT, DH], BF16)
+            nc.sync.dma_start(out=q_sb[:], in_=q[b, h].rearrange("(t p) d -> p t d", p=P))
+            k_sb = unit_loads.tile([P, NT, DH], BF16)
+            nc.sync.dma_start(out=k_sb[:], in_=k1[b, h].rearrange("(t p) d -> p t d", p=P))
+            kept[unit, "q_sb"], kept[unit, "k_sb"] = q_sb, k_sb
 
         def transpose_features(b, half):
             kv_words = kept[b, "kv_sb"][:].bitcast(F32)
@@ -151,12 +158,11 @@ def tile_attention_pa_t_kernel(tc, q, k1, key_values_input, Wv1_words, Wv1_scale
             )
 
         def transpose_qk(unit):
-            b, h = divmod(unit, H)
             qkT_ps = scratch.tile([P, 2 * NT, P], BF16, tag="scratch")
             for t in range(NT):
-                nc.tensor.transpose(qkT_ps[:, t, :], kept[b, "q_sb"][:, h * NT + t, :], ident_bf[:])
+                nc.tensor.transpose(qkT_ps[:, t, :], kept[unit, "q_sb"][:, t, :], ident_bf[:])
             for t in range(NT):
-                nc.tensor.transpose(qkT_ps[:, NT + t, :], kept[b, "k_sb"][:, h * NT + t, :], ident_bf[:])
+                nc.tensor.transpose(qkT_ps[:, NT + t, :], kept[unit, "k_sb"][:, t, :], ident_bf[:])
             kept[unit, "qkT_ps"] = qkT_ps
 
         def copy_qk(unit):
@@ -164,57 +170,52 @@ def tile_attention_pa_t_kernel(tc, q, k1, key_values_input, Wv1_words, Wv1_scale
             nc.vector.tensor_copy(out=qkT[:], in_=kept[unit, "qkT_ps"][:].rearrange("p t i -> p (t i)"))
             kept[unit, "qkT"] = qkT
 
-        def logits(unit, half):
+        def logits(unit, it):
             qkT = kept[unit, "qkT"]
-            for it in range(2 * half, 2 * half + 2):
-                s_ps = logit_banks.tile([P, NT, P], F32)
-                nc.tensor.matmul(
-                    out=s_ps[:].rearrange("p a j -> p (a j)"),
-                    lhsT=qkT[:, it * P : (it + 1) * P],
-                    rhs=qkT[:, N : 2 * N],
-                    start=True,
-                    stop=False,
-                )
-                masked_tiles = min(2, NT - it)
-                for a in range(masked_tiles):
-                    nc.tensor.matmul(
-                        out=s_ps[:, it + a, :], lhsT=mask_T[:, a, :], rhs=ident_f32[:], is_transpose=True,
-                        start=False, stop=(a == masked_tiles - 1),
-                    )
-                kept[unit, "s_ps", it] = s_ps
-
-        def maxima(unit, half):
-            if half == 0:
-                s_max = small.tile([P, NT], F32)
-                kept[unit, "s_max"] = s_max
-            for it in range(2 * half, 2 * half + 2):
-                nc.vector.tensor_reduce(
-                    out=kept[unit, "s_max"][:, it : it + 1], in_=kept[unit, "s_ps", it][:], axis=AXIS.XY, op=ALU.max
-                )
-
-        def finish_max(unit):
-            h = unit % H
-            neg_m = small.tile([P, NT], F32)
-            nc.vector.tensor_scalar(
-                out=neg_m[:], in0=kept[unit, "s_max"][:], scalar1=-SCALE, scalar2=neg_sink[:, h : h + 1],
-                op0=ALU.mult, op1=ALU.min,
+            s_ps = logit_banks.tile([P, NT, P], F32)
+            nc.tensor.matmul(
+                out=s_ps[:].rearrange("p a j -> p (a j)"),
+                lhsT=qkT[:, it * P : (it + 1) * P],
+                rhs=qkT[:, N : 2 * N],
+                start=True,
+                stop=False,
             )
-            kept[unit, "neg_m"] = neg_m
+            masked_tiles = min(2, NT - it)
+            for a in range(masked_tiles):
+                nc.tensor.matmul(
+                    out=s_ps[:, it + a, :], lhsT=mask_T[:, a, :], rhs=ident_f32[:], is_transpose=True,
+                    start=False, stop=(a == masked_tiles - 1),
+                )
+            kept[unit, "s_ps", it] = s_ps
 
-        def exponentials(unit, half):
+        def maximum(unit, it):
+            h = unit % H
+            if it == 0:
+                s_max = small.tile([P, NT], F32)
+                neg_m = small.tile([P, NT], F32)
+                kept[unit, "s_max"], kept[unit, "neg_m"] = s_max, neg_m
+            column = slice(it, it + 1)
+            nc.vector.tensor_reduce(
+                out=kept[unit, "s_max"][:, column], in_=kept[unit, "s_ps", it][:], axis=AXIS.XY, op=ALU.max
+            )
+            nc.vector.tensor_scalar(
+                out=kept[unit, "neg_m"][:, column], in0=kept[unit, "s_max"][:, column], scalar1=-SCALE,
+                scalar2=neg_sink[:, h : h + 1], op0=ALU.mult, op1=ALU.min,
+            )
+
+        def exponential(unit, it):
             h = unit % H
             neg_m = kept[unit, "neg_m"]
-            if half == 0:
+            if it == 0:
                 e_sb = work.tile([P, NT, N], BF16)
                 den_parts = small.tile([P, NT, 2], F32)
                 kept[unit, "e_sb"], kept[unit, "den_parts"] = e_sb, den_parts
             e_sb, den_parts = kept[unit, "e_sb"], kept[unit, "den_parts"]
-            for it in range(2 * half, 2 * half + 2):
-                nc.scalar.activation(
-                    out=e_sb[:, it, :], in_=kept[unit, "s_ps", it][:].rearrange("p a j -> p (a j)"), func=FUNC.Exp,
-                    bias=neg_m[:, it : it + 1], scale=SCALE, accum_out=den_parts[:, it, 0:1],
-                )
-            if half == 1:
+            nc.scalar.activation(
+                out=e_sb[:, it, :], in_=kept[unit, "s_ps", it][:].rearrange("p a j -> p (a j)"), func=FUNC.Exp,
+                bias=neg_m[:, it : it + 1], scale=SCALE, accum_out=den_parts[:, it, 0:1],
+            )
+            if it == NT - 1:
                 nc.scalar.activation(
                     out=den_parts[:, :, 1], in_=neg_m[:], func=FUNC.Exp, bias=sink[:, h : h + 1], scale=1.0
                 )
@@ -248,35 +249,39 @@ def tile_attention_pa_t_kernel(tc, q, k1, key_values_input, Wv1_words, Wv1_scale
                 in_=kept[unit, "eT_ps", half][:].rearrange("p t u i -> p t i u"),
             )
 
-        def quantise_e(unit):
-            e_codes = work.tile([P, N], U32, align_bytes=64)
-            e_scales = work.tile([P, N], U8, align_bytes=64)
+        def quantise_e(unit, half):
+            if half == 0:
+                e_codes = work.tile([P, N], U32, align_bytes=64)
+                e_scales = work.tile([P, N], U8, align_bytes=64)
+                kept[unit, "e_codes"], kept[unit, "e_scales"] = e_codes, e_scales
+            queries = slice(half * 2 * P, (half + 1) * 2 * P)
             nc.vector.quantize_mx(
-                out=e_codes[:].bitcast(FP8X4), scales=e_scales[:], in_=kept[unit, "e_grouped"][:]
+                out=kept[unit, "e_codes"][:, queries].bitcast(FP8X4),
+                scales=kept[unit, "e_scales"][:, queries],
+                in_=kept[unit, "e_grouped"][:, half * 2 * P * PACK : (half + 1) * 2 * P * PACK],
             )
-            kept[unit, "e_codes"], kept[unit, "e_scales"] = e_codes, e_scales
 
-        def weighted_values(unit):
+        def weighted_values(unit, half):
             b, h = divmod(unit, H)
             head = slice(h * DV, (h + 1) * DV)
-            for half in range(2):
-                acc = sums.tile([P, 2, DV], F32)
-                for t2 in range(2):
-                    rows = slice((2 * half + t2) * P, (2 * half + t2 + 1) * P)
-                    nc.tensor.matmul_mx(
-                        out=acc[:, t2, :],
-                        lhsT=kept[unit, "e_codes"][:, rows].bitcast(FP8X4),
-                        lhsT_scale=kept[unit, "e_scales"][:, rows],
-                        rhs=kept[b, "v_codes"][:, head].bitcast(FP8X4),
-                        rhs_scale=kept[b, "v_scales"][:, head],
-                        start=True,
-                        stop=True,
-                    )
-                kept[unit, "acc", half] = acc
-            tanh_sb = results.tile([P, NT, DV], F32)
-            gate = results.tile([P, NT, DV], F32)
-            o_sb = results.tile([P, NT, DV], F32)
-            kept[unit, "tanh_sb"], kept[unit, "gate"], kept[unit, "o_sb"] = tanh_sb, gate, o_sb
+            acc = sums.tile([P, 2, DV], F32)
+            for t2 in range(2):
+                rows = slice((2 * half + t2) * P, (2 * half + t2 + 1) * P)
+                nc.tensor.matmul_mx(
+                    out=acc[:, t2, :],
+                    lhsT=kept[unit, "e_codes"][:, rows].bitcast(FP8X4),
+                    lhsT_scale=kept[unit, "e_scales"][:, rows],
+                    rhs=kept[b, "v_codes"][:, head].bitcast(FP8X4),
+                    rhs_scale=kept[b, "v_scales"][:, head],
+                    start=True,
+                    stop=True,
+                )
+            kept[unit, "acc", half] = acc
+            if half == 0:
+                tanh_sb = results.tile([P, NT, DV], F32)
+                gate = results.tile([P, NT, DV], F32)
+                o_sb = results.tile([P, NT, DV], F32)
+                kept[unit, "tanh_sb"], kept[unit, "gate"], kept[unit, "o_sb"] = tanh_sb, gate, o_sb
 
         def tanh_gate(unit, half):
             half_inv_den = kept[unit, "half_inv_den"]
@@ -298,9 +303,12 @@ def tile_attention_pa_t_kernel(tc, q, k1, key_values_input, Wv1_words, Wv1_scale
                 in1=kept[unit, "gate"][:, pair, :], op=ALU.mult,
             )
 
-        def store(unit):
+        def store(unit, half):
             b, h = divmod(unit, H)
-            nc.sync.dma_start(out=out[b, h].rearrange("(t p) c -> p t c", p=P), in_=kept[unit, "o_sb"][:])
+            nc.sync.dma_start(
+                out=out[b, h, half * 2 * P : (half + 1) * 2 * P, :].rearrange("(t p) c -> p t c", p=P),
+                in_=kept[unit, "o_sb"][:, 2 * half : 2 * half + 2, :],
+            )
 
         def when_live(stage, unit, *args):
             if 0 <= unit < UNITS:
@@ -310,28 +318,31 @@ def tile_attention_pa_t_kernel(tc, q, k1, key_values_input, Wv1_words, Wv1_scale
             if 0 <= unit < UNITS and unit % H == 0:
                 stage(unit // H, *args)
 
-        load_sequence(0)
+        load_qk(0)
+        load_features(0)
         nc.sync.dma_start(
             out=w_codes[:].bitcast(I32), in_=Wv1_words[0].rearrange("p n t -> p (n t)").bitcast(I32)
         )
+        load_qk(1)
         for n in range(-4, UNITS + 2):
+            when_live(load_qk, n + QK_AHEAD)
             if n % H == 0 and n // H + 2 < B:
-                load_sequence(n // H + 2)
-            when_live(finish, n - 2, 0)
-            when_live(finish, n - 2, 1)
-            when_live(store, n - 2)
-            when_live(exponentials, n, 0)
-            when_live(logits, n + 1, 0)
-            when_live(round_values, n + 1, 0)
-            when_live(transpose_e, n, 0)
-            when_live(exponentials, n, 1)
-            when_live(logits, n + 1, 1)
+                load_features(n // H + 2)
+            for half in range(2):
+                when_live(finish, n - 2, half)
+                when_live(store, n - 2, half)
+            for it in range(NT):
+                when_live(exponential, n, it)
+                ahead, it_ahead = divmod(n * NT + it + LOGIT_BANKS, NT)
+                when_live(logits, ahead, it_ahead)
+                when_live(maximum, ahead, it_ahead)
+                if it == 1:
+                    when_live(round_values, n + 1, 0)
+                    when_live(transpose_e, n, 0)
             when_live(round_values, n + 1, 1)
             when_live(transpose_e, n, 1)
-            when_live(weighted_values, n - 1)
-            when_live(maxima, n + 1, 0)
-            when_live(maxima, n + 1, 1)
-            when_live(finish_max, n + 1)
+            when_live(weighted_values, n - 1, 0)
+            when_live(weighted_values, n - 1, 1)
             when_live(tanh_gate, n - 1, 0)
             when_live(group_e, n, 0)
             when_live(transpose_qk, n + 2)
@@ -340,7 +351,8 @@ def tile_attention_pa_t_kernel(tc, q, k1, key_values_input, Wv1_words, Wv1_scale
             when_live(project, n + 2, 0)
             when_live(denominators, n)
             when_live(quantise_values, n + 1)
-            when_live(quantise_e, n)
+            when_live(quantise_e, n, 0)
+            when_live(quantise_e, n, 1)
             when_live(copy_qk, n + 2)
             when_first_head(transpose_features, n + 4, 0)
             when_first_head(transpose_features, n + 3, 1)

@@ -45,13 +45,6 @@ def tile_attention_pa_t_kernel(tc, q, k1, key_values_input, Wv1_words, Wv1_scale
         w_codes = const.tile([P, DM], U32, align_bytes=64)
         w_scales = const.tile([P, DM], U8, align_bytes=64)
         nc.vector.memset(w_scales[:].bitcast(I32), 0)
-        for quad in range(4):
-            nc.sync.dma_start(
-                out=w_scales[32 * quad : 32 * quad + 4, :].bitcast(I32),
-                in_=Wv1_scales[0, 4 * quad : 4 * quad + 4, :].bitcast(I32),
-            )
-        sink_bf = const.tile([P, H], BF16)
-        nc.sync.dma_start(out=sink_bf[:], in_=attn_sink.partition_broadcast(P))
 
         ident_f32 = const.tile([P, P], F32)
         make_identity(nc, ident_f32[:])
@@ -69,10 +62,9 @@ def tile_attention_pa_t_kernel(tc, q, k1, key_values_input, Wv1_words, Wv1_scale
             fill=-FLT_MAX, base=-1, channel_multiplier=1,
         )
 
+        sink_bf = const.tile([P, H], BF16)
         sink = const.tile([P, H], F32)
-        nc.vector.tensor_copy(out=sink[:], in_=sink_bf[:])
         neg_sink = const.tile([P, H], F32)
-        nc.vector.tensor_scalar(out=neg_sink[:], in0=sink[:], scalar1=-1.0, scalar2=None, op0=ALU.mult)
 
         kept = {}
 
@@ -107,7 +99,7 @@ def tile_attention_pa_t_kernel(tc, q, k1, key_values_input, Wv1_words, Wv1_scale
                 kv_grouped = values.tile([P, N * PACK], BF16, align_bytes=64)
                 kept[b, "kv_grouped"] = kv_grouped
             kv_grouped_words = kept[b, "kv_grouped"][:].bitcast(F32).rearrange("p (t j u) -> p t j u", t=NT, u=2)
-            nc.vector.tensor_copy(
+            nc.scalar.copy(
                 out=kv_grouped_words[:, 2 * half : 2 * half + 2],
                 in_=kept[b, "kvT_ps", half][:].rearrange("p t u j -> p t j u"),
             )
@@ -146,7 +138,10 @@ def tile_attention_pa_t_kernel(tc, q, k1, key_values_input, Wv1_words, Wv1_scale
             first = (2 * h + piece) * P * PACK
             grouped = kept[b, "v_grouped"][:, first : first + P * PACK].rearrange("p (n t) -> p n t", t=PACK)
             by_column = kept[unit, "v_ps", piece][:].rearrange("p t n -> p n t")
-            nc.scalar.copy(out=grouped, in_=by_column)
+            if piece == 0:
+                nc.vector.tensor_copy(out=grouped, in_=by_column)
+            else:
+                nc.scalar.copy(out=grouped, in_=by_column)
 
         def quantise_values(unit):
             b, h = divmod(unit, H)
@@ -319,7 +314,15 @@ def tile_attention_pa_t_kernel(tc, q, k1, key_values_input, Wv1_words, Wv1_scale
                 stage(unit // H, *args)
 
         load_qk(0)
+        nc.sync.dma_start(out=sink_bf[:], in_=attn_sink.partition_broadcast(P))
+        nc.vector.tensor_copy(out=sink[:], in_=sink_bf[:])
+        nc.vector.tensor_scalar(out=neg_sink[:], in0=sink[:], scalar1=-1.0, scalar2=None, op0=ALU.mult)
         load_features(0)
+        for quad in range(4):
+            nc.sync.dma_start(
+                out=w_scales[32 * quad : 32 * quad + 4, :].bitcast(I32),
+                in_=Wv1_scales[0, 4 * quad : 4 * quad + 4, :].bitcast(I32),
+            )
         nc.sync.dma_start(
             out=w_codes[:].bitcast(I32), in_=Wv1_words[0].rearrange("p n t -> p (n t)").bitcast(I32)
         )

@@ -22,8 +22,9 @@ SCALE = DH ** -0.5
 FLT_MAX = 3.4028234663852886e38
 
 UNITS = B * H
-QK_AHEAD = 6
-LOGIT_BANKS = 3
+GROUP = 2 * H
+FIRST_TANH = UNITS - GROUP
+LOGIT_BANKS = 4
 
 FLOPS = 2 * B * N * DKV * DM + 2 * B * H * N * N * DH + 2 * B * H * N * N * DV
 
@@ -33,14 +34,17 @@ def tile_attention_pa_t_kernel(tc, q, k1, key_values_input, Wv1_words, Wv1_scale
     with ExitStack() as stack:
         const = stack.enter_context(tc.tile_pool(name="const", bufs=1))
         loads = stack.enter_context(tc.tile_pool(name="loads", bufs=3))
-        unit_loads = stack.enter_context(tc.tile_pool(name="unit_loads", bufs=QK_AHEAD + 1))
-        values = stack.enter_context(tc.tile_pool(name="values", bufs=2))
+        unit_loads = stack.enter_context(tc.tile_pool(name="unit_loads", bufs=GROUP + 2))
+        features = stack.enter_context(tc.tile_pool(name="features", bufs=3))
+        values = stack.enter_context(tc.tile_pool(name="values", bufs=GROUP * 2 + 2))
+        prepared = stack.enter_context(tc.tile_pool(name="prepared", bufs=GROUP + 2))
         work = stack.enter_context(tc.tile_pool(name="work", bufs=3))
-        results = stack.enter_context(tc.tile_pool(name="results", bufs=3))
-        small = stack.enter_context(tc.tile_pool(name="small", bufs=4))
+        results = stack.enter_context(tc.tile_pool(name="results", bufs=4))
+        gates = stack.enter_context(tc.tile_pool(name="gates", bufs=2))
+        small = stack.enter_context(tc.tile_pool(name="small", bufs=GROUP + 4))
         logit_banks = stack.enter_context(tc.psum_pool(name="logit_banks", bufs=LOGIT_BANKS))
-        scratch = stack.enter_context(tc.psum_pool(name="scratch", bufs=3))
-        sums = stack.enter_context(tc.psum_pool(name="sums", bufs=2))
+        turned = stack.enter_context(tc.psum_pool(name="turned", bufs=2))
+        side = stack.enter_context(tc.psum_pool(name="side", bufs=2))
 
         w_codes = const.tile([P, DM], U32, align_bytes=64)
         w_scales = const.tile([P, DM], U8, align_bytes=64)
@@ -66,6 +70,10 @@ def tile_attention_pa_t_kernel(tc, q, k1, key_values_input, Wv1_words, Wv1_scale
         sink = const.tile([P, H], F32)
         neg_sink = const.tile([P, H], F32)
 
+        warm = const.tile([P, 1], F32)
+        nc.vector.memset(warm[:], 0.0)
+        nc.scalar.activation(out=warm[:], in_=warm[:], func=FUNC.Exp)
+
         kept = {}
 
         def load_features(b):
@@ -84,9 +92,9 @@ def tile_attention_pa_t_kernel(tc, q, k1, key_values_input, Wv1_words, Wv1_scale
             nc.sync.dma_start(out=k_sb[:], in_=k1[b, h].rearrange("(t p) d -> p t d", p=P))
             kept[unit, "q_sb"], kept[unit, "k_sb"] = q_sb, k_sb
 
-        def transpose_features(b, half):
+        def transpose_features(b, half, bank_pool):
             kv_words = kept[b, "kv_sb"][:].bitcast(F32)
-            kvT_ps = scratch.tile([P, 2, 2, P], F32, tag="scratch")
+            kvT_ps = bank_pool.tile([P, 2, 2, P], F32, tag="bank")
             for t2 in range(2):
                 for u in range(2):
                     nc.tensor.transpose(
@@ -94,32 +102,28 @@ def tile_attention_pa_t_kernel(tc, q, k1, key_values_input, Wv1_words, Wv1_scale
                     )
             kept[b, "kvT_ps", half] = kvT_ps
 
-        def group_features(b, half):
+        def group_features(b, half, copy):
             if half == 0:
-                kv_grouped = values.tile([P, N * PACK], BF16, align_bytes=64)
+                kv_grouped = loads.tile([P, N * PACK], BF16, align_bytes=64)
                 kept[b, "kv_grouped"] = kv_grouped
             kv_grouped_words = kept[b, "kv_grouped"][:].bitcast(F32).rearrange("p (t j u) -> p t j u", t=NT, u=2)
-            nc.scalar.copy(
+            copy(
                 out=kv_grouped_words[:, 2 * half : 2 * half + 2],
                 in_=kept[b, "kvT_ps", half][:].rearrange("p t u j -> p t j u"),
             )
 
         def quantise_features(b):
-            kv_codes = values.tile([P, N], U32, align_bytes=64)
-            kv_scales = values.tile([P, N], U8, align_bytes=64)
+            kv_codes = features.tile([P, N], U32, align_bytes=64)
+            kv_scales = features.tile([P, N], U8, align_bytes=64)
             nc.vector.quantize_mx(
                 out=kv_codes[:].bitcast(FP8X4), scales=kv_scales[:], in_=kept[b, "kv_grouped"][:]
             )
-            v_grouped = values.tile([P, DM * PACK], BF16, align_bytes=64)
-            v_codes = values.tile([P, DM], U32, align_bytes=64)
-            v_scales = values.tile([P, DM], U8, align_bytes=64)
             kept[b, "kv_codes"], kept[b, "kv_scales"] = kv_codes, kv_scales
-            kept[b, "v_grouped"], kept[b, "v_codes"], kept[b, "v_scales"] = v_grouped, v_codes, v_scales
 
-        def project(unit, piece):
+        def project(unit, piece, bank_pool):
             b, h = divmod(unit, H)
             cols = slice((2 * h + piece) * P, (2 * h + piece + 1) * P)
-            v_ps = scratch.tile([P, NT, P], F32, tag="scratch")
+            v_ps = bank_pool.tile([P, NT, P], F32, tag="bank")
             for t in range(NT):
                 rows = slice(t * P, (t + 1) * P)
                 nc.tensor.matmul_mx(
@@ -133,27 +137,28 @@ def tile_attention_pa_t_kernel(tc, q, k1, key_values_input, Wv1_words, Wv1_scale
                 )
             kept[unit, "v_ps", piece] = v_ps
 
-        def round_values(unit, piece):
-            b, h = divmod(unit, H)
-            first = (2 * h + piece) * P * PACK
-            grouped = kept[b, "v_grouped"][:, first : first + P * PACK].rearrange("p (n t) -> p n t", t=PACK)
-            by_column = kept[unit, "v_ps", piece][:].rearrange("p t n -> p n t")
-            if piece == 0:
-                nc.vector.tensor_copy(out=grouped, in_=by_column)
-            else:
-                nc.scalar.copy(out=grouped, in_=by_column)
+        def round_values(unit, piece, copy):
+            v_grouped = work.tile([P, P * PACK], BF16, align_bytes=64)
+            copy(
+                out=v_grouped[:].rearrange("p (n t) -> p n t", t=PACK),
+                in_=kept[unit, "v_ps", piece][:].rearrange("p t n -> p n t"),
+            )
+            kept[unit, "v_grouped", piece] = v_grouped
 
-        def quantise_values(unit):
-            b, h = divmod(unit, H)
-            head = slice(h * DV, (h + 1) * DV)
+        def quantise_values(unit, piece):
+            if (unit, "v_codes") not in kept:
+                v_codes = values.tile([P, DV], U32, align_bytes=64)
+                v_scales = values.tile([P, DV], U8, align_bytes=64)
+                kept[unit, "v_codes"], kept[unit, "v_scales"] = v_codes, v_scales
+            cols = slice(piece * P, (piece + 1) * P)
             nc.vector.quantize_mx(
-                out=kept[b, "v_codes"][:, head].bitcast(FP8X4),
-                scales=kept[b, "v_scales"][:, head],
-                in_=kept[b, "v_grouped"][:, h * DV * PACK : (h + 1) * DV * PACK],
+                out=kept[unit, "v_codes"][:, cols].bitcast(FP8X4),
+                scales=kept[unit, "v_scales"][:, cols],
+                in_=kept[unit, "v_grouped", piece][:],
             )
 
-        def transpose_qk(unit):
-            qkT_ps = scratch.tile([P, 2 * NT, P], BF16, tag="scratch")
+        def transpose_qk(unit, bank_pool):
+            qkT_ps = bank_pool.tile([P, 2 * NT, P], BF16, tag="bank")
             for t in range(NT):
                 nc.tensor.transpose(qkT_ps[:, t, :], kept[unit, "q_sb"][:, t, :], ident_bf[:])
             for t in range(NT):
@@ -161,13 +166,13 @@ def tile_attention_pa_t_kernel(tc, q, k1, key_values_input, Wv1_words, Wv1_scale
             kept[unit, "qkT_ps"] = qkT_ps
 
         def copy_qk(unit):
-            qkT = work.tile([P, 2 * N], BF16)
+            qkT = prepared.tile([P, 2 * N], BF16)
             nc.vector.tensor_copy(out=qkT[:], in_=kept[unit, "qkT_ps"][:].rearrange("p t i -> p (t i)"))
             kept[unit, "qkT"] = qkT
 
         def logits(unit, it):
             qkT = kept[unit, "qkT"]
-            s_ps = logit_banks.tile([P, NT, P], F32)
+            s_ps = logit_banks.tile([P, NT, P], F32, tag="bank")
             nc.tensor.matmul(
                 out=s_ps[:].rearrange("p a j -> p (a j)"),
                 lhsT=qkT[:, it * P : (it + 1) * P],
@@ -193,7 +198,7 @@ def tile_attention_pa_t_kernel(tc, q, k1, key_values_input, Wv1_words, Wv1_scale
             nc.vector.tensor_reduce(
                 out=kept[unit, "s_max"][:, column], in_=kept[unit, "s_ps", it][:], axis=AXIS.XY, op=ALU.max
             )
-            nc.vector.tensor_scalar(
+            nc.gpsimd.tensor_scalar(
                 out=kept[unit, "neg_m"][:, column], in0=kept[unit, "s_max"][:, column], scalar1=-SCALE,
                 scalar2=neg_sink[:, h : h + 1], op0=ALU.mult, op1=ALU.min,
             )
@@ -216,17 +221,25 @@ def tile_attention_pa_t_kernel(tc, q, k1, key_values_input, Wv1_words, Wv1_scale
                 )
 
         def denominators(unit):
+            den_parts = kept[unit, "den_parts"]
             den = small.tile([P, NT], F32)
-            nc.vector.tensor_reduce(out=den[:], in_=kept[unit, "den_parts"][:], axis=AXIS.X, op=ALU.add)
+            nc.gpsimd.tensor_tensor(out=den[:], in0=den_parts[:, :, 0], in1=den_parts[:, :, 1], op=ALU.add)
+            kept[unit, "den"] = den
+
+        def invert(unit):
             inv_den = small.tile([P, NT], F32)
-            nc.vector.reciprocal(out=inv_den[:], in_=den[:])
-            half_inv_den = small.tile([P, NT], F32)
-            nc.vector.tensor_scalar(out=half_inv_den[:], in0=inv_den[:], scalar1=0.5, scalar2=None, op0=ALU.mult)
-            kept[unit, "half_inv_den"] = half_inv_den
+            nc.vector.reciprocal(out=inv_den[:], in_=kept[unit, "den"][:])
+            kept[unit, "inv_den"] = inv_den
+            if unit >= FIRST_TANH:
+                half_inv_den = small.tile([P, NT], F32)
+                nc.gpsimd.tensor_scalar(
+                    out=half_inv_den[:], in0=inv_den[:], scalar1=0.5, scalar2=None, op0=ALU.mult
+                )
+                kept[unit, "half_inv_den"] = half_inv_den
 
         def transpose_e(unit, half):
             e_words = kept[unit, "e_sb"][:].bitcast(F32)
-            eT_ps = scratch.tile([P, 2, 2, P], F32, tag="scratch")
+            eT_ps = turned.tile([P, 2, 2, P], F32, tag="bank")
             for t2 in range(2):
                 for u in range(2):
                     nc.tensor.transpose(
@@ -246,8 +259,8 @@ def tile_attention_pa_t_kernel(tc, q, k1, key_values_input, Wv1_words, Wv1_scale
 
         def quantise_e(unit, half):
             if half == 0:
-                e_codes = work.tile([P, N], U32, align_bytes=64)
-                e_scales = work.tile([P, N], U8, align_bytes=64)
+                e_codes = prepared.tile([P, N], U32, align_bytes=64)
+                e_scales = prepared.tile([P, N], U8, align_bytes=64)
                 kept[unit, "e_codes"], kept[unit, "e_scales"] = e_codes, e_scales
             queries = slice(half * 2 * P, (half + 1) * 2 * P)
             nc.vector.quantize_mx(
@@ -256,30 +269,38 @@ def tile_attention_pa_t_kernel(tc, q, k1, key_values_input, Wv1_words, Wv1_scale
                 in_=kept[unit, "e_grouped"][:, half * 2 * P * PACK : (half + 1) * 2 * P * PACK],
             )
 
-        def weighted_values(unit, half):
-            b, h = divmod(unit, H)
-            head = slice(h * DV, (h + 1) * DV)
-            acc = sums.tile([P, 2, DV], F32)
+        def weighted_values(unit, half, bank_pool):
+            acc = bank_pool.tile([P, 2, DV], F32, tag="bank")
             for t2 in range(2):
                 rows = slice((2 * half + t2) * P, (2 * half + t2 + 1) * P)
                 nc.tensor.matmul_mx(
                     out=acc[:, t2, :],
                     lhsT=kept[unit, "e_codes"][:, rows].bitcast(FP8X4),
                     lhsT_scale=kept[unit, "e_scales"][:, rows],
-                    rhs=kept[b, "v_codes"][:, head].bitcast(FP8X4),
-                    rhs_scale=kept[b, "v_scales"][:, head],
+                    rhs=kept[unit, "v_codes"][:].bitcast(FP8X4),
+                    rhs_scale=kept[unit, "v_scales"][:],
                     start=True,
                     stop=True,
                 )
             kept[unit, "acc", half] = acc
             if half == 0:
-                tanh_sb = results.tile([P, NT, DV], F32)
-                gate = results.tile([P, NT, DV], F32)
                 o_sb = results.tile([P, NT, DV], F32)
-                kept[unit, "tanh_sb"], kept[unit, "gate"], kept[unit, "o_sb"] = tanh_sb, gate, o_sb
+                kept[unit, "o_sb"] = o_sb
+
+        def silu(unit, half):
+            for t2 in range(2):
+                it = 2 * half + t2
+                nc.scalar.activation(
+                    out=kept[unit, "o_sb"][:, it, :], in_=kept[unit, "acc", half][:, t2, :], func=FUNC.Silu,
+                    scale=kept[unit, "inv_den"][:, it : it + 1],
+                )
 
         def tanh_gate(unit, half):
             half_inv_den = kept[unit, "half_inv_den"]
+            if half == 0:
+                tanh_sb = gates.tile([P, NT, DV], F32)
+                gate = gates.tile([P, NT, DV], F32)
+                kept[unit, "tanh_sb"], kept[unit, "gate"] = tanh_sb, gate
             for t2 in range(2):
                 it = 2 * half + t2
                 nc.scalar.activation(
@@ -305,15 +326,44 @@ def tile_attention_pa_t_kernel(tc, q, k1, key_values_input, Wv1_words, Wv1_scale
                 in_=kept[unit, "o_sb"][:, 2 * half : 2 * half + 2, :],
             )
 
-        def when_live(stage, unit, *args):
-            if 0 <= unit < UNITS:
-                stage(unit, *args)
+        def qk_job(unit, bank_pool):
+            return [lambda: transpose_qk(unit, bank_pool), lambda: copy_qk(unit)]
 
-        def when_first_head(stage, unit, *args):
-            if 0 <= unit < UNITS and unit % H == 0:
-                stage(unit // H, *args)
+        def value_job(unit, piece, bank_pool, copy):
+            return [
+                lambda: project(unit, piece, bank_pool),
+                lambda: round_values(unit, piece, copy),
+                lambda: quantise_values(unit, piece),
+            ]
+
+        def feature_jobs(b, bank_pool, copy):
+            return [
+                [lambda: transpose_features(b, 0, bank_pool), lambda: group_features(b, 0, copy)],
+                [
+                    lambda: transpose_features(b, 1, bank_pool),
+                    lambda: group_features(b, 1, copy),
+                    lambda: quantise_features(b),
+                ],
+            ]
+
+        under_way = []
+
+        def advance():
+            for stages in reversed(list(under_way)):
+                stages.pop(0)()
+                if not stages:
+                    under_way.remove(stages)
+
+        def begin(job):
+            job.pop(0)()
+            under_way.append(job)
+
+        def place(slots, jobs, begin_at, end_at):
+            for i, job in enumerate(jobs):
+                slots[begin_at + i * (end_at - begin_at) // len(jobs)].append(job)
 
         load_qk(0)
+        load_qk(1)
         nc.sync.dma_start(out=sink_bf[:], in_=attn_sink.partition_broadcast(P))
         nc.vector.tensor_copy(out=sink[:], in_=sink_bf[:])
         nc.vector.tensor_scalar(out=neg_sink[:], in0=sink[:], scalar1=-1.0, scalar2=None, op0=ALU.mult)
@@ -326,40 +376,134 @@ def tile_attention_pa_t_kernel(tc, q, k1, key_values_input, Wv1_words, Wv1_scale
         nc.sync.dma_start(
             out=w_codes[:].bitcast(I32), in_=Wv1_words[0].rearrange("p n t -> p (n t)").bitcast(I32)
         )
-        load_qk(1)
-        for n in range(-4, UNITS + 2):
-            when_live(load_qk, n + QK_AHEAD)
-            if n % H == 0 and n // H + 2 < B:
-                load_features(n // H + 2)
-            for half in range(2):
-                when_live(finish, n - 2, half)
-                when_live(store, n - 2, half)
-            for it in range(NT):
-                when_live(exponential, n, it)
-                ahead, it_ahead = divmod(n * NT + it + LOGIT_BANKS, NT)
-                when_live(logits, ahead, it_ahead)
-                when_live(maximum, ahead, it_ahead)
-                if it == 1:
-                    when_live(round_values, n + 1, 0)
-                    when_live(transpose_e, n, 0)
-            when_live(round_values, n + 1, 1)
-            when_live(transpose_e, n, 1)
-            when_live(weighted_values, n - 1, 0)
-            when_live(weighted_values, n - 1, 1)
-            when_live(tanh_gate, n - 1, 0)
-            when_live(group_e, n, 0)
-            when_live(transpose_qk, n + 2)
-            when_live(tanh_gate, n - 1, 1)
-            when_live(group_e, n, 1)
-            when_live(project, n + 2, 0)
-            when_live(denominators, n)
-            when_live(quantise_values, n + 1)
-            when_live(quantise_e, n, 0)
-            when_live(quantise_e, n, 1)
-            when_live(copy_qk, n + 2)
-            when_first_head(transpose_features, n + 4, 0)
-            when_first_head(transpose_features, n + 3, 1)
-            when_first_head(group_features, n + 4, 0)
-            when_first_head(group_features, n + 3, 1)
-            when_live(project, n + 2, 1)
-            when_first_head(quantise_features, n + 3)
+        load_qk(2)
+        load_features(1)
+        load_qk(3)
+
+        stack.enter_context(tc.manual_schedule())
+        V, S = nc.vector.tensor_copy, nc.scalar.copy
+        transpose_qk(0, side)
+        copy_qk(0)
+        transpose_qk(1, side)
+        for it in range(LOGIT_BANKS):
+            logits(0, it)
+            maximum(0, it)
+        copy_qk(1)
+
+        def values_of(units, bank_pool, copies):
+            return [value_job(unit, piece, bank_pool, copies[piece]) for unit in units for piece in range(2)]
+
+        for first in range(0, UNITS, GROUP):
+            group = range(first, first + GROUP)
+            last = group[-1]
+            b = first // H
+            with_tanh = first >= FIRST_TANH
+            bank_pool = logit_banks if with_tanh else side
+            lead = LOGIT_BANKS - 1 if with_tanh else LOGIT_BANKS
+            qk_jobs = [qk_job(unit + 2, bank_pool) for unit in group if unit + 2 < UNITS]
+            if first == 0:
+                others = feature_jobs(0, side, S) + values_of(range(0, H), side, (V, S)) + feature_jobs(1, side, S) + feature_jobs(2, side, S)
+            elif with_tanh:
+                others = feature_jobs(b + 1, bank_pool, V) + values_of(range(first + H, first + 2 * H), bank_pool, (V, V))
+            else:
+                others = feature_jobs(b + 1, side, V) + feature_jobs(b + 2, side, V)
+            if not with_tanh:
+                burst_jobs = values_of(range(first + H, first + 3 * H), logit_banks, (V, V))
+            slots = [[] for step in range(GROUP * NT)]
+            place(slots, qk_jobs, 1, 1 + NT * len(qk_jobs))
+            place(slots, others, 0, GROUP * NT)
+            for unit in group:
+                if unit + 4 < UNITS:
+                    load_qk(unit + 4)
+                if unit % H == 0 and unit // H + 2 < B:
+                    load_features(unit // H + 2)
+                for it in range(NT):
+                    if it == 0 and unit > first:
+                        transpose_e(unit - 1, 1)
+                    if it == 2:
+                        transpose_e(unit, 0)
+                    exponential(unit, it)
+                    if with_tanh:
+                        if it == 0 and unit > first + 1:
+                            tanh_gate(unit - 2, 1)
+                        if it == 2 and unit > first:
+                            tanh_gate(unit - 1, 0)
+                    if it == 1 and unit > first:
+                        group_e(unit - 1, 1)
+                    if it == 3:
+                        group_e(unit, 0)
+                        denominators(unit)
+                    advance()
+                    if unit > first:
+                        if it == 0:
+                            quantise_e(unit - 1, 0)
+                            invert(unit - 1)
+                        if it == 2:
+                            quantise_e(unit - 1, 1)
+                    if with_tanh:
+                        if it == 0 and unit > first + 1:
+                            finish(unit - 2, 0)
+                            store(unit - 2, 0)
+                        if it == 2 and unit > first + 1:
+                            finish(unit - 2, 1)
+                            store(unit - 2, 1)
+                    ahead, it_ahead = divmod(unit * NT + it + lead, NT)
+                    if ahead <= last:
+                        logits(ahead, it_ahead)
+                        maximum(ahead, it_ahead)
+                    elif not with_tanh:
+                        begin(burst_jobs.pop(0))
+                    if with_tanh and unit > first:
+                        if it == 1:
+                            weighted_values(unit - 1, 0, side)
+                        if it == 3:
+                            weighted_values(unit - 1, 1, side)
+                    for job in slots[(unit - first) * NT + it]:
+                        begin(job)
+            transpose_e(last, 1)
+            advance()
+            if with_tanh:
+                tanh_gate(last - 1, 1)
+                quantise_e(last, 0)
+                invert(last)
+                finish(last - 1, 0)
+                store(last - 1, 0)
+                group_e(last, 1)
+                weighted_values(last, 0, side)
+                tanh_gate(last, 0)
+                finish(last - 1, 1)
+                store(last - 1, 1)
+                quantise_e(last, 1)
+                weighted_values(last, 1, side)
+                finish(last, 0)
+                store(last, 0)
+                tanh_gate(last, 1)
+                finish(last, 1)
+                store(last, 1)
+            else:
+                quantise_e(last, 0)
+                invert(last)
+                halves = [(unit, half) for unit in group for half in range(2)]
+                slots = [[] for step in range(len(halves) - 2)]
+                place(slots, burst_jobs, 0, len(halves) - 2)
+                AHEAD = 3
+                for i in range(AHEAD):
+                    weighted_values(*halves[i], (side, turned)[i % 2])
+                for i, (unit, half) in enumerate(halves):
+                    silu(unit, half)
+                    store(unit, half)
+                    if i == 0:
+                        group_e(last, 1)
+                    advance()
+                    if i == 1:
+                        quantise_e(last, 1)
+                    if i + AHEAD < len(halves):
+                        weighted_values(*halves[i + AHEAD], (side, turned)[(i + AHEAD) % 2])
+                    if i < len(slots):
+                        for job in slots[i]:
+                            begin(job)
+                    else:
+                        for it in range(2 * half, 2 * half + 2):
+                            if it < (LOGIT_BANKS - 1 if last + 1 >= FIRST_TANH else LOGIT_BANKS):
+                                logits(last + 1, it)
+                                maximum(last + 1, it)

@@ -19,7 +19,7 @@ P = 128
 NT = N // P
 PACK = 4
 SCALE = DH ** -0.5
-FLT_MAX = 3.4028234663852886e38
+MASKED = -(2.0**127)
 
 UNITS = B * H
 GROUP = 2 * H
@@ -55,15 +55,19 @@ def tile_attention_pa_t_kernel(tc, q, k1, key_values_input, Wv1_words, Wv1_scale
         ident_bf = const.tile([P, P], BF16)
         make_identity(nc, ident_bf[:])
 
-        mask_T = const.tile([P, 2, P], F32)
-        nc.gpsimd.memset(mask_T[:], 0.0)
+        mask_f32 = const.tile([P, P], F32)
+        nc.gpsimd.memset(mask_f32[:], 0.0)
         nc.gpsimd.affine_select(
-            out=mask_T[:, 0, :], in_=mask_T[:, 0, :], pattern=[[1, P]], compare_op=ALU.is_ge,
-            fill=-FLT_MAX, base=0, channel_multiplier=-1,
+            out=mask_f32[:], in_=mask_f32[:], pattern=[[-1, P]], compare_op=ALU.is_ge,
+            fill=MASKED, base=0, channel_multiplier=1,
         )
+        mask_own = const.tile([P, P], BF16)
+        nc.vector.tensor_copy(out=mask_own[:], in_=mask_f32[:])
+        mask_next_T = const.tile([P, P], F32)
+        nc.gpsimd.memset(mask_next_T[:], 0.0)
         nc.gpsimd.affine_select(
-            out=mask_T[:, 1, :], in_=mask_T[:, 1, :], pattern=[[-1, P]], compare_op=ALU.is_ge,
-            fill=-FLT_MAX, base=-1, channel_multiplier=1,
+            out=mask_next_T[:], in_=mask_next_T[:], pattern=[[-1, P]], compare_op=ALU.is_ge,
+            fill=MASKED, base=-1, channel_multiplier=1,
         )
 
         sink_bf = const.tile([P, H], BF16)
@@ -180,11 +184,13 @@ def tile_attention_pa_t_kernel(tc, q, k1, key_values_input, Wv1_words, Wv1_scale
                 start=True,
                 stop=False,
             )
-            masked_tiles = min(2, NT - it)
-            for a in range(masked_tiles):
+            nc.tensor.matmul(
+                out=s_ps[:, it, :], lhsT=ident_bf[:], rhs=mask_own[:], start=False, stop=(it == NT - 1)
+            )
+            if it < NT - 1:
                 nc.tensor.matmul(
-                    out=s_ps[:, it + a, :], lhsT=mask_T[:, a, :], rhs=ident_f32[:], is_transpose=True,
-                    start=False, stop=(a == masked_tiles - 1),
+                    out=s_ps[:, it + 1, :], lhsT=mask_next_T[:], rhs=ident_f32[:], is_transpose=True,
+                    start=False, stop=True,
                 )
             kept[unit, "s_ps", it] = s_ps
 

@@ -1,3 +1,4 @@
+import math
 from contextlib import ExitStack
 
 import concourse.mybir as mybir
@@ -22,9 +23,8 @@ SCALE = DH ** -0.5
 MASKED = -(2.0**127)
 
 UNITS = B * H
-GROUP = 2 * H
-FIRST_TANH = UNITS - GROUP
-LOGIT_BANKS = 4
+QK_AHEAD = 6
+LOGIT_BANKS = 3
 
 FLOPS = 2 * B * N * DKV * DM + 2 * B * H * N * N * DH + 2 * B * H * N * N * DV
 
@@ -34,17 +34,15 @@ def tile_attention_pa_t_kernel(tc, q, k1, key_values_input, Wv1_words, Wv1_scale
     with ExitStack() as stack:
         const = stack.enter_context(tc.tile_pool(name="const", bufs=1))
         loads = stack.enter_context(tc.tile_pool(name="loads", bufs=3))
-        unit_loads = stack.enter_context(tc.tile_pool(name="unit_loads", bufs=GROUP + 2))
-        features = stack.enter_context(tc.tile_pool(name="features", bufs=3))
-        values = stack.enter_context(tc.tile_pool(name="values", bufs=GROUP * 2 + 2))
-        prepared = stack.enter_context(tc.tile_pool(name="prepared", bufs=GROUP + 2))
+        unit_loads = stack.enter_context(tc.tile_pool(name="unit_loads", bufs=QK_AHEAD + 1))
+        values = stack.enter_context(tc.tile_pool(name="values", bufs=4))
         work = stack.enter_context(tc.tile_pool(name="work", bufs=3))
-        results = stack.enter_context(tc.tile_pool(name="results", bufs=4))
-        gates = stack.enter_context(tc.tile_pool(name="gates", bufs=2))
-        small = stack.enter_context(tc.tile_pool(name="small", bufs=GROUP + 4))
+        results = stack.enter_context(tc.tile_pool(name="results", bufs=3))
+        small = stack.enter_context(tc.tile_pool(name="small", bufs=4))
         logit_banks = stack.enter_context(tc.psum_pool(name="logit_banks", bufs=LOGIT_BANKS))
-        turned = stack.enter_context(tc.psum_pool(name="turned", bufs=2))
+        turned = stack.enter_context(tc.psum_pool(name="turned", bufs=1))
         side = stack.enter_context(tc.psum_pool(name="side", bufs=2))
+        sums = stack.enter_context(tc.psum_pool(name="sums", bufs=2))
 
         w_codes = const.tile([P, DM], U32, align_bytes=64)
         w_scales = const.tile([P, DM], U8, align_bytes=64)
@@ -73,6 +71,7 @@ def tile_attention_pa_t_kernel(tc, q, k1, key_values_input, Wv1_words, Wv1_scale
         sink_bf = const.tile([P, H], BF16)
         sink = const.tile([P, H], F32)
         neg_sink = const.tile([P, H], F32)
+        sink_ln2 = const.tile([P, H], F32)
 
         warm = const.tile([P, 1], F32)
         nc.vector.memset(warm[:], 0.0)
@@ -96,9 +95,9 @@ def tile_attention_pa_t_kernel(tc, q, k1, key_values_input, Wv1_words, Wv1_scale
             nc.sync.dma_start(out=k_sb[:], in_=k1[b, h].rearrange("(t p) d -> p t d", p=P))
             kept[unit, "q_sb"], kept[unit, "k_sb"] = q_sb, k_sb
 
-        def transpose_features(b, half, bank_pool):
+        def transpose_features(b, half):
             kv_words = kept[b, "kv_sb"][:].bitcast(F32)
-            kvT_ps = bank_pool.tile([P, 2, 2, P], F32, tag="bank")
+            kvT_ps = side.tile([P, 2, 2, P], F32, tag="bank")
             for t2 in range(2):
                 for u in range(2):
                     nc.tensor.transpose(
@@ -106,28 +105,28 @@ def tile_attention_pa_t_kernel(tc, q, k1, key_values_input, Wv1_words, Wv1_scale
                     )
             kept[b, "kvT_ps", half] = kvT_ps
 
-        def group_features(b, half, copy):
+        def group_features(b, half):
             if half == 0:
                 kv_grouped = loads.tile([P, N * PACK], BF16, align_bytes=64)
                 kept[b, "kv_grouped"] = kv_grouped
             kv_grouped_words = kept[b, "kv_grouped"][:].bitcast(F32).rearrange("p (t j u) -> p t j u", t=NT, u=2)
-            copy(
+            nc.scalar.copy(
                 out=kv_grouped_words[:, 2 * half : 2 * half + 2],
                 in_=kept[b, "kvT_ps", half][:].rearrange("p t u j -> p t j u"),
             )
 
         def quantise_features(b):
-            kv_codes = features.tile([P, N], U32, align_bytes=64)
-            kv_scales = features.tile([P, N], U8, align_bytes=64)
+            kv_codes = values.tile([P, N], U32, align_bytes=64)
+            kv_scales = values.tile([P, N], U8, align_bytes=64)
             nc.vector.quantize_mx(
                 out=kv_codes[:].bitcast(FP8X4), scales=kv_scales[:], in_=kept[b, "kv_grouped"][:]
             )
             kept[b, "kv_codes"], kept[b, "kv_scales"] = kv_codes, kv_scales
 
-        def project(unit, piece, bank_pool):
+        def project(unit, piece):
             b, h = divmod(unit, H)
             cols = slice((2 * h + piece) * P, (2 * h + piece + 1) * P)
-            v_ps = bank_pool.tile([P, NT, P], F32, tag="bank")
+            v_ps = side.tile([P, NT, P], F32, tag="bank")
             for t in range(NT):
                 rows = slice(t * P, (t + 1) * P)
                 nc.tensor.matmul_mx(
@@ -141,28 +140,28 @@ def tile_attention_pa_t_kernel(tc, q, k1, key_values_input, Wv1_words, Wv1_scale
                 )
             kept[unit, "v_ps", piece] = v_ps
 
-        def round_values(unit, piece, copy):
-            v_grouped = work.tile([P, P * PACK], BF16, align_bytes=64)
-            copy(
-                out=v_grouped[:].rearrange("p (n t) -> p n t", t=PACK),
-                in_=kept[unit, "v_ps", piece][:].rearrange("p t n -> p n t"),
-            )
-            kept[unit, "v_grouped", piece] = v_grouped
+        def round_values(unit, piece):
+            if piece == 0:
+                v_grouped = work.tile([P, DV * PACK], BF16, align_bytes=64)
+                kept[unit, "v_grouped"] = v_grouped
+            first = piece * P * PACK
+            grouped = kept[unit, "v_grouped"][:, first : first + P * PACK].rearrange("p (n t) -> p n t", t=PACK)
+            by_column = kept[unit, "v_ps", piece][:].rearrange("p t n -> p n t")
+            if piece == 0:
+                nc.vector.tensor_copy(out=grouped, in_=by_column)
+            else:
+                nc.scalar.copy(out=grouped, in_=by_column)
 
-        def quantise_values(unit, piece):
-            if (unit, "v_codes") not in kept:
-                v_codes = values.tile([P, DV], U32, align_bytes=64)
-                v_scales = values.tile([P, DV], U8, align_bytes=64)
-                kept[unit, "v_codes"], kept[unit, "v_scales"] = v_codes, v_scales
-            cols = slice(piece * P, (piece + 1) * P)
+        def quantise_values(unit):
+            v_codes = values.tile([P, DV], U32, align_bytes=64)
+            v_scales = values.tile([P, DV], U8, align_bytes=64)
+            kept[unit, "v_codes"], kept[unit, "v_scales"] = v_codes, v_scales
             nc.vector.quantize_mx(
-                out=kept[unit, "v_codes"][:, cols].bitcast(FP8X4),
-                scales=kept[unit, "v_scales"][:, cols],
-                in_=kept[unit, "v_grouped", piece][:],
+                out=v_codes[:].bitcast(FP8X4), scales=v_scales[:], in_=kept[unit, "v_grouped"][:]
             )
 
-        def transpose_qk(unit, bank_pool):
-            qkT_ps = bank_pool.tile([P, 2 * NT, P], BF16, tag="bank")
+        def transpose_qk(unit):
+            qkT_ps = side.tile([P, 2 * NT, P], BF16, tag="bank")
             for t in range(NT):
                 nc.tensor.transpose(qkT_ps[:, t, :], kept[unit, "q_sb"][:, t, :], ident_bf[:])
             for t in range(NT):
@@ -170,7 +169,7 @@ def tile_attention_pa_t_kernel(tc, q, k1, key_values_input, Wv1_words, Wv1_scale
             kept[unit, "qkT_ps"] = qkT_ps
 
         def copy_qk(unit):
-            qkT = prepared.tile([P, 2 * N], BF16)
+            qkT = work.tile([P, 2 * N], BF16)
             nc.vector.tensor_copy(out=qkT[:], in_=kept[unit, "qkT_ps"][:].rearrange("p t i -> p (t i)"))
             kept[unit, "qkT"] = qkT
 
@@ -195,7 +194,6 @@ def tile_attention_pa_t_kernel(tc, q, k1, key_values_input, Wv1_words, Wv1_scale
             kept[unit, "s_ps", it] = s_ps
 
         def maximum(unit, it):
-            h = unit % H
             if it == 0:
                 s_max = small.tile([P, NT], F32)
                 neg_m = small.tile([P, NT], F32)
@@ -204,6 +202,10 @@ def tile_attention_pa_t_kernel(tc, q, k1, key_values_input, Wv1_words, Wv1_scale
             nc.vector.tensor_reduce(
                 out=kept[unit, "s_max"][:, column], in_=kept[unit, "s_ps", it][:], axis=AXIS.XY, op=ALU.max
             )
+
+        def negate(unit, it):
+            h = unit % H
+            column = slice(it, it + 1)
             nc.gpsimd.tensor_scalar(
                 out=kept[unit, "neg_m"][:, column], in0=kept[unit, "s_max"][:, column], scalar1=-SCALE,
                 scalar2=neg_sink[:, h : h + 1], op0=ALU.mult, op1=ALU.min,
@@ -223,25 +225,22 @@ def tile_attention_pa_t_kernel(tc, q, k1, key_values_input, Wv1_words, Wv1_scale
             )
             if it == NT - 1:
                 nc.scalar.activation(
-                    out=den_parts[:, :, 1], in_=neg_m[:], func=FUNC.Exp, bias=sink[:, h : h + 1], scale=1.0
+                    out=den_parts[:, :, 1], in_=neg_m[:], func=FUNC.Exp, bias=sink_ln2[:, h : h + 1], scale=1.0
                 )
 
         def denominators(unit):
             den_parts = kept[unit, "den_parts"]
-            den = small.tile([P, NT], F32)
-            nc.gpsimd.tensor_tensor(out=den[:], in0=den_parts[:, :, 0], in1=den_parts[:, :, 1], op=ALU.add)
-            kept[unit, "den"] = den
+            twice_den = small.tile([P, NT], F32)
+            nc.vector.scalar_tensor_tensor(
+                out=twice_den[:], in0=den_parts[:, :, 0], scalar=2.0, in1=den_parts[:, :, 1],
+                op0=ALU.mult, op1=ALU.add,
+            )
+            kept[unit, "twice_den"] = twice_den
 
         def invert(unit):
-            inv_den = small.tile([P, NT], F32)
-            nc.vector.reciprocal(out=inv_den[:], in_=kept[unit, "den"][:])
-            kept[unit, "inv_den"] = inv_den
-            if unit >= FIRST_TANH:
-                half_inv_den = small.tile([P, NT], F32)
-                nc.gpsimd.tensor_scalar(
-                    out=half_inv_den[:], in0=inv_den[:], scalar1=0.5, scalar2=None, op0=ALU.mult
-                )
-                kept[unit, "half_inv_den"] = half_inv_den
+            half_inv_den = small.tile([P, NT], F32)
+            nc.vector.reciprocal(out=half_inv_den[:], in_=kept[unit, "twice_den"][:])
+            kept[unit, "half_inv_den"] = half_inv_den
 
         def transpose_e(unit, half):
             e_words = kept[unit, "e_sb"][:].bitcast(F32)
@@ -265,8 +264,8 @@ def tile_attention_pa_t_kernel(tc, q, k1, key_values_input, Wv1_words, Wv1_scale
 
         def quantise_e(unit, half):
             if half == 0:
-                e_codes = prepared.tile([P, N], U32, align_bytes=64)
-                e_scales = prepared.tile([P, N], U8, align_bytes=64)
+                e_codes = work.tile([P, N], U32, align_bytes=64)
+                e_scales = work.tile([P, N], U8, align_bytes=64)
                 kept[unit, "e_codes"], kept[unit, "e_scales"] = e_codes, e_scales
             queries = slice(half * 2 * P, (half + 1) * 2 * P)
             nc.vector.quantize_mx(
@@ -275,8 +274,8 @@ def tile_attention_pa_t_kernel(tc, q, k1, key_values_input, Wv1_words, Wv1_scale
                 in_=kept[unit, "e_grouped"][:, half * 2 * P * PACK : (half + 1) * 2 * P * PACK],
             )
 
-        def weighted_values(unit, half, bank_pool):
-            acc = bank_pool.tile([P, 2, DV], F32, tag="bank")
+        def weighted_values(unit, half):
+            acc = sums.tile([P, 2, DV], F32, tag="bank")
             for t2 in range(2):
                 rows = slice((2 * half + t2) * P, (2 * half + t2 + 1) * P)
                 nc.tensor.matmul_mx(
@@ -293,19 +292,11 @@ def tile_attention_pa_t_kernel(tc, q, k1, key_values_input, Wv1_words, Wv1_scale
                 o_sb = results.tile([P, NT, DV], F32)
                 kept[unit, "o_sb"] = o_sb
 
-        def silu(unit, half):
-            for t2 in range(2):
-                it = 2 * half + t2
-                nc.scalar.activation(
-                    out=kept[unit, "o_sb"][:, it, :], in_=kept[unit, "acc", half][:, t2, :], func=FUNC.Silu,
-                    scale=kept[unit, "inv_den"][:, it : it + 1],
-                )
-
         def tanh_gate(unit, half):
             half_inv_den = kept[unit, "half_inv_den"]
             if half == 0:
-                tanh_sb = gates.tile([P, NT, DV], F32)
-                gate = gates.tile([P, NT, DV], F32)
+                tanh_sb = results.tile([P, NT, DV], F32)
+                gate = results.tile([P, NT, DV], F32)
                 kept[unit, "tanh_sb"], kept[unit, "gate"] = tanh_sb, gate
             for t2 in range(2):
                 it = 2 * half + t2
@@ -332,47 +323,26 @@ def tile_attention_pa_t_kernel(tc, q, k1, key_values_input, Wv1_words, Wv1_scale
                 in_=kept[unit, "o_sb"][:, 2 * half : 2 * half + 2, :],
             )
 
-        def qk_job(unit, bank_pool):
-            return [lambda: transpose_qk(unit, bank_pool), lambda: copy_qk(unit)]
+        def when_live(stage, unit, *args):
+            if 0 <= unit < UNITS:
+                stage(unit, *args)
 
-        def value_job(unit, piece, bank_pool, copy):
-            return [
-                lambda: project(unit, piece, bank_pool),
-                lambda: round_values(unit, piece, copy),
-                lambda: quantise_values(unit, piece),
-            ]
+        def when_first_head(stage, unit, *args):
+            if 0 <= unit < UNITS and unit % H == 0:
+                stage(unit // H, *args)
 
-        def feature_jobs(b, bank_pool, copy):
-            return [
-                [lambda: transpose_features(b, 0, bank_pool), lambda: group_features(b, 0, copy)],
-                [
-                    lambda: transpose_features(b, 1, bank_pool),
-                    lambda: group_features(b, 1, copy),
-                    lambda: quantise_features(b),
-                ],
-            ]
+        def search(tile):
+            when_live(maximum, *divmod(tile, NT))
 
-        under_way = []
-
-        def advance():
-            for stages in reversed(list(under_way)):
-                stages.pop(0)()
-                if not stages:
-                    under_way.remove(stages)
-
-        def begin(job):
-            job.pop(0)()
-            under_way.append(job)
-
-        def place(slots, jobs, begin_at, end_at):
-            for i, job in enumerate(jobs):
-                slots[begin_at + i * (end_at - begin_at) // len(jobs)].append(job)
+        def negated(tile):
+            when_live(negate, *divmod(tile, NT))
 
         load_qk(0)
         load_qk(1)
         nc.sync.dma_start(out=sink_bf[:], in_=attn_sink.partition_broadcast(P))
         nc.vector.tensor_copy(out=sink[:], in_=sink_bf[:])
         nc.vector.tensor_scalar(out=neg_sink[:], in0=sink[:], scalar1=-1.0, scalar2=None, op0=ALU.mult)
+        nc.vector.tensor_scalar(out=sink_ln2[:], in0=sink[:], scalar1=math.log(2.0), scalar2=None, op0=ALU.add)
         load_features(0)
         for quad in range(4):
             nc.sync.dma_start(
@@ -387,129 +357,83 @@ def tile_attention_pa_t_kernel(tc, q, k1, key_values_input, Wv1_words, Wv1_scale
         load_qk(3)
 
         stack.enter_context(tc.manual_schedule())
-        V, S = nc.vector.tensor_copy, nc.scalar.copy
-        transpose_qk(0, side)
+        transpose_qk(0)
         copy_qk(0)
-        transpose_qk(1, side)
+        transpose_qk(1)
         for it in range(LOGIT_BANKS):
             logits(0, it)
             maximum(0, it)
+            negate(0, it)
         copy_qk(1)
+        for n in range(UNITS + 2):
+            when_live(load_qk, n + 4)
+            if n % H == 0 and n // H + 2 < B:
+                load_features(n // H + 2)
+            T = n * NT + LOGIT_BANKS
 
-        def values_of(units, bank_pool, copies):
-            return [value_job(unit, piece, bank_pool, copies[piece]) for unit in units for piece in range(2)]
+            when_live(transpose_e, n - 1, 1)
+            when_live(exponential, n, 0)
+            if n == 0:
+                transpose_features(0, 0)
+                group_features(0, 0)
+                transpose_features(0, 1)
+            else:
+                when_live(round_values, n, 1)
+            when_live(group_e, n - 1, 1)
+            when_live(logits, *divmod(T, NT))
+            when_live(invert, n - 1)
+            if n >= 1:
+                when_live(copy_qk, n + 1)
+            search(T)
+            negated(T)
+            when_live(weighted_values, n - 1, 0)
+            if n > 0:
+                when_live(project, n + 1, 0)
 
-        for first in range(0, UNITS, GROUP):
-            group = range(first, first + GROUP)
-            last = group[-1]
-            b = first // H
-            with_tanh = first >= FIRST_TANH
-            bank_pool = logit_banks if with_tanh else side
-            lead = LOGIT_BANKS - 1 if with_tanh else LOGIT_BANKS
-            qk_jobs = [qk_job(unit + 2, bank_pool) for unit in group if unit + 2 < UNITS]
-            if first == 0:
-                others = feature_jobs(0, side, S) + values_of(range(0, H), side, (V, S)) + feature_jobs(1, side, S) + feature_jobs(2, side, S)
-            elif with_tanh:
-                others = feature_jobs(b + 1, bank_pool, V) + values_of(range(first + H, first + 2 * H), bank_pool, (V, V))
-            else:
-                others = feature_jobs(b + 1, side, V) + feature_jobs(b + 2, side, V)
-            if not with_tanh:
-                burst_jobs = values_of(range(first + H, first + 3 * H), logit_banks, (V, V))
-            slots = [[] for step in range(GROUP * NT)]
-            place(slots, qk_jobs, 1, 1 + NT * len(qk_jobs))
-            place(slots, others, 0, GROUP * NT)
-            for unit in group:
-                if unit + 4 < UNITS:
-                    load_qk(unit + 4)
-                if unit % H == 0 and unit // H + 2 < B:
-                    load_features(unit // H + 2)
-                for it in range(NT):
-                    if it == 0 and unit > first:
-                        transpose_e(unit - 1, 1)
-                    if it == 2:
-                        transpose_e(unit, 0)
-                    exponential(unit, it)
-                    if with_tanh:
-                        if it == 0 and unit > first + 1:
-                            tanh_gate(unit - 2, 1)
-                        if it == 2 and unit > first:
-                            tanh_gate(unit - 1, 0)
-                    if it == 1 and unit > first:
-                        group_e(unit - 1, 1)
-                    if it == 3:
-                        group_e(unit, 0)
-                        denominators(unit)
-                    advance()
-                    if unit > first:
-                        if it == 0:
-                            quantise_e(unit - 1, 0)
-                            invert(unit - 1)
-                        if it == 2:
-                            quantise_e(unit - 1, 1)
-                    if with_tanh:
-                        if it == 0 and unit > first + 1:
-                            finish(unit - 2, 0)
-                            store(unit - 2, 0)
-                        if it == 2 and unit > first + 1:
-                            finish(unit - 2, 1)
-                            store(unit - 2, 1)
-                    ahead, it_ahead = divmod(unit * NT + it + lead, NT)
-                    if ahead <= last:
-                        logits(ahead, it_ahead)
-                        maximum(ahead, it_ahead)
-                    elif not with_tanh:
-                        begin(burst_jobs.pop(0))
-                    if with_tanh and unit > first:
-                        if it == 1:
-                            weighted_values(unit - 1, 0, side)
-                        if it == 3:
-                            weighted_values(unit - 1, 1, side)
-                    for job in slots[(unit - first) * NT + it]:
-                        begin(job)
-            transpose_e(last, 1)
-            advance()
-            if with_tanh:
-                tanh_gate(last - 1, 1)
-                quantise_e(last, 0)
-                invert(last)
-                finish(last - 1, 0)
-                store(last - 1, 0)
-                group_e(last, 1)
-                weighted_values(last, 0, side)
-                tanh_gate(last, 0)
-                finish(last - 1, 1)
-                store(last - 1, 1)
-                quantise_e(last, 1)
-                weighted_values(last, 1, side)
-                finish(last, 0)
-                store(last, 0)
-                tanh_gate(last, 1)
-                finish(last, 1)
-                store(last, 1)
-            else:
-                quantise_e(last, 0)
-                invert(last)
-                halves = [(unit, half) for unit in group for half in range(2)]
-                slots = [[] for step in range(len(halves) - 2)]
-                place(slots, burst_jobs, 0, len(halves) - 2)
-                AHEAD = 3
-                for i in range(AHEAD):
-                    weighted_values(*halves[i], (side, turned)[i % 2])
-                for i, (unit, half) in enumerate(halves):
-                    silu(unit, half)
-                    store(unit, half)
-                    if i == 0:
-                        group_e(last, 1)
-                    advance()
-                    if i == 1:
-                        quantise_e(last, 1)
-                    if i + AHEAD < len(halves):
-                        weighted_values(*halves[i + AHEAD], (side, turned)[(i + AHEAD) % 2])
-                    if i < len(slots):
-                        for job in slots[i]:
-                            begin(job)
-                    else:
-                        for it in range(2 * half, 2 * half + 2):
-                            if it < (LOGIT_BANKS - 1 if last + 1 >= FIRST_TANH else LOGIT_BANKS):
-                                logits(last + 1, it)
-                                maximum(last + 1, it)
+            when_live(exponential, n, 1)
+            if n == 0:
+                group_features(0, 1)
+                quantise_features(0)
+            when_live(tanh_gate, n - 1, 0)
+            when_first_head(transpose_features, n + 3, 0)
+            when_first_head(transpose_features, n + 2, 1)
+            when_live(logits, *divmod(T + 1, NT))
+            when_live(finish, n - 2, 1)
+            when_live(store, n - 2, 1)
+            when_live(quantise_e, n - 1, 1)
+            search(T + 1)
+            negated(T + 1)
+
+            when_live(transpose_e, n, 0)
+            when_live(exponential, n, 2)
+            when_first_head(group_features, n + 3, 0)
+            when_first_head(group_features, n + 2, 1)
+            when_live(group_e, n, 0)
+            when_live(logits, *divmod(T + 2, NT))
+            if n == 0:
+                project(0, 0)
+                project(0, 1)
+                round_values(0, 0)
+                round_values(0, 1)
+            if n > 0:
+                when_live(round_values, n + 1, 0)
+            when_live(quantise_values, n)
+            search(T + 2)
+            negated(T + 2)
+            when_live(weighted_values, n - 1, 1)
+            when_live(project, n + 1, 0 if n == 0 else 1)
+
+            when_live(exponential, n, 3)
+            if n == 0:
+                round_values(1, 0)
+                project(1, 1)
+            when_live(tanh_gate, n - 1, 1)
+            when_live(logits, *divmod(T + 3, NT))
+            when_live(finish, n - 1, 0)
+            when_live(store, n - 1, 0)
+            when_live(denominators, n)
+            when_live(quantise_e, n, 0)
+            when_first_head(quantise_features, n + 2)
+            search(T + 3)
+            negated(T + 3)
+            when_live(transpose_qk, n + 2)

@@ -44,6 +44,10 @@ def tile_attention_pa_t_kernel(tc, q, k1, key_values_input, Wv1_words, Wv1_scale
         side = stack.enter_context(tc.psum_pool(name="side", bufs=2))
         sums = stack.enter_context(tc.psum_pool(name="sums", bufs=2))
 
+        warm = const.tile([P, 1], F32)
+        nc.vector.memset(warm[:], 0.0)
+        nc.scalar.activation(out=warm[:], in_=warm[:], func=FUNC.Exp)
+
         w_codes = const.tile([P, DM], U32, align_bytes=64)
         w_scales = const.tile([P, DM], U8, align_bytes=64)
         nc.vector.memset(w_scales[:].bitcast(I32), 0)
@@ -72,10 +76,6 @@ def tile_attention_pa_t_kernel(tc, q, k1, key_values_input, Wv1_words, Wv1_scale
         sink = const.tile([P, H], F32)
         neg_sink = const.tile([P, H], F32)
         sink_ln2 = const.tile([P, H], F32)
-
-        warm = const.tile([P, 1], F32)
-        nc.vector.memset(warm[:], 0.0)
-        nc.scalar.activation(out=warm[:], in_=warm[:], func=FUNC.Exp)
 
         kept = {}
 
@@ -115,13 +115,17 @@ def tile_attention_pa_t_kernel(tc, q, k1, key_values_input, Wv1_words, Wv1_scale
                 in_=kept[b, "kvT_ps", half][:].rearrange("p t u j -> p t j u"),
             )
 
-        def quantise_features(b):
-            kv_codes = values.tile([P, N], U32, align_bytes=64)
-            kv_scales = values.tile([P, N], U8, align_bytes=64)
+        def quantise_features(b, half):
+            if half == 0:
+                kv_codes = values.tile([P, N], U32, align_bytes=64)
+                kv_scales = values.tile([P, N], U8, align_bytes=64)
+                kept[b, "kv_codes"], kept[b, "kv_scales"] = kv_codes, kv_scales
+            keys = slice(half * 2 * P, (half + 1) * 2 * P)
             nc.vector.quantize_mx(
-                out=kv_codes[:].bitcast(FP8X4), scales=kv_scales[:], in_=kept[b, "kv_grouped"][:]
+                out=kept[b, "kv_codes"][:, keys].bitcast(FP8X4),
+                scales=kept[b, "kv_scales"][:, keys],
+                in_=kept[b, "kv_grouped"][:, half * 2 * P * PACK : (half + 1) * 2 * P * PACK],
             )
-            kept[b, "kv_codes"], kept[b, "kv_scales"] = kv_codes, kv_scales
 
         def project(unit, piece):
             b, h = divmod(unit, H)
@@ -147,10 +151,7 @@ def tile_attention_pa_t_kernel(tc, q, k1, key_values_input, Wv1_words, Wv1_scale
             first = piece * P * PACK
             grouped = kept[unit, "v_grouped"][:, first : first + P * PACK].rearrange("p (n t) -> p n t", t=PACK)
             by_column = kept[unit, "v_ps", piece][:].rearrange("p t n -> p n t")
-            if piece == 0:
-                nc.vector.tensor_copy(out=grouped, in_=by_column)
-            else:
-                nc.scalar.copy(out=grouped, in_=by_column)
+            nc.vector.tensor_copy(out=grouped, in_=by_column)
 
         def quantise_values(unit):
             v_codes = values.tile([P, DV], U32, align_bytes=64)
@@ -170,7 +171,7 @@ def tile_attention_pa_t_kernel(tc, q, k1, key_values_input, Wv1_words, Wv1_scale
 
         def copy_qk(unit):
             qkT = work.tile([P, 2 * N], BF16)
-            nc.vector.tensor_copy(out=qkT[:], in_=kept[unit, "qkT_ps"][:].rearrange("p t i -> p (t i)"))
+            nc.scalar.copy(out=qkT[:], in_=kept[unit, "qkT_ps"][:].rearrange("p t i -> p (t i)"))
             kept[unit, "qkT"] = qkT
 
         def logits(unit, it):
@@ -293,27 +294,28 @@ def tile_attention_pa_t_kernel(tc, q, k1, key_values_input, Wv1_words, Wv1_scale
                 kept[unit, "o_sb"] = o_sb
 
         def tanh_gate(unit, half):
-            half_inv_den = kept[unit, "half_inv_den"]
             if half == 0:
                 tanh_sb = results.tile([P, NT, DV], F32)
-                gate = results.tile([P, NT, DV], F32)
-                kept[unit, "tanh_sb"], kept[unit, "gate"] = tanh_sb, gate
+                blend = results.tile([P, NT, DV], F32)
+                kept[unit, "tanh_sb"], kept[unit, "blend"] = tanh_sb, blend
             for t2 in range(2):
                 it = 2 * half + t2
                 nc.scalar.activation(
                     out=kept[unit, "tanh_sb"][:, it, :], in_=kept[unit, "acc", half][:, t2, :], func=FUNC.Tanh,
-                    scale=half_inv_den[:, it : it + 1],
-                )
-                nc.gpsimd.tensor_scalar(
-                    out=kept[unit, "gate"][:, it, :], in0=kept[unit, "tanh_sb"][:, it, :], scalar1=1.0,
-                    scalar2=half_inv_den[:, it : it + 1], op0=ALU.add, op1=ALU.mult,
+                    scale=kept[unit, "half_inv_den"][:, it : it + 1],
                 )
 
         def finish(unit, half):
             pair = slice(2 * half, 2 * half + 2)
-            nc.vector.tensor_tensor(
-                out=kept[unit, "o_sb"][:, pair, :], in0=kept[unit, "acc", half][:],
-                in1=kept[unit, "gate"][:, pair, :], op=ALU.mult,
+            nc.vector.scalar_tensor_tensor(
+                out=kept[unit, "blend"][:, pair, :], in0=kept[unit, "tanh_sb"][:, pair, :], scalar=1.0,
+                in1=kept[unit, "acc", half][:], op0=ALU.add, op1=ALU.mult,
+            )
+
+        def divide(unit, it):
+            nc.gpsimd.tensor_scalar(
+                out=kept[unit, "o_sb"][:, it, :], in0=kept[unit, "blend"][:, it, :],
+                scalar1=kept[unit, "half_inv_den"][:, it : it + 1], scalar2=0.0, op0=ALU.mult, op1=ALU.add,
             )
 
         def store(unit, half):
@@ -359,81 +361,77 @@ def tile_attention_pa_t_kernel(tc, q, k1, key_values_input, Wv1_words, Wv1_scale
         stack.enter_context(tc.manual_schedule())
         transpose_qk(0)
         copy_qk(0)
+        transpose_features(0, 0)
+        group_features(0, 0)
+        logits(0, 0)
+        maximum(0, 0)
+        negate(0, 0)
+        logits(0, 1)
+        maximum(0, 1)
+        negate(0, 1)
+        transpose_features(0, 1)
+        group_features(0, 1)
         transpose_qk(1)
-        for it in range(LOGIT_BANKS):
-            logits(0, it)
-            maximum(0, it)
-            negate(0, it)
-        copy_qk(1)
+        quantise_features(0, 0)
+        logits(0, 2)
+        maximum(0, 2)
+        negate(0, 2)
+        quantise_features(0, 1)
         for n in range(UNITS + 2):
             when_live(load_qk, n + 4)
             if n % H == 0 and n // H + 2 < B:
                 load_features(n // H + 2)
             T = n * NT + LOGIT_BANKS
 
-            when_live(transpose_e, n - 1, 1)
             when_live(exponential, n, 0)
-            if n == 0:
-                transpose_features(0, 0)
-                group_features(0, 0)
-                transpose_features(0, 1)
-            else:
-                when_live(round_values, n, 1)
+            when_live(copy_qk, n + 1)
             when_live(group_e, n - 1, 1)
             when_live(logits, *divmod(T, NT))
-            when_live(invert, n - 1)
-            if n >= 1:
-                when_live(copy_qk, n + 1)
+            when_live(finish, n - 2, 1)
             search(T)
             negated(T)
+            when_live(divide, n - 2, 2)
             when_live(weighted_values, n - 1, 0)
-            if n > 0:
-                when_live(project, n + 1, 0)
+            when_live(project, n, 0)
 
             when_live(exponential, n, 1)
-            if n == 0:
-                group_features(0, 1)
-                quantise_features(0)
             when_live(tanh_gate, n - 1, 0)
-            when_first_head(transpose_features, n + 3, 0)
-            when_first_head(transpose_features, n + 2, 1)
+            when_live(transpose_e, n, 0)
             when_live(logits, *divmod(T + 1, NT))
-            when_live(finish, n - 2, 1)
-            when_live(store, n - 2, 1)
+            when_live(round_values, n, 0)
             when_live(quantise_e, n - 1, 1)
             search(T + 1)
             negated(T + 1)
+            when_live(divide, n - 2, 3)
+            when_live(store, n - 2, 1)
+            when_live(project, n, 1)
 
-            when_live(transpose_e, n, 0)
             when_live(exponential, n, 2)
-            when_first_head(group_features, n + 3, 0)
-            when_first_head(group_features, n + 2, 1)
             when_live(group_e, n, 0)
+            when_first_head(transpose_features, n + 4, 0)
+            when_first_head(transpose_features, n + 3, 1)
             when_live(logits, *divmod(T + 2, NT))
-            if n == 0:
-                project(0, 0)
-                project(0, 1)
-                round_values(0, 0)
-                round_values(0, 1)
-            if n > 0:
-                when_live(round_values, n + 1, 0)
-            when_live(quantise_values, n)
+            when_live(finish, n - 1, 0)
+            when_live(round_values, n, 1)
             search(T + 2)
             negated(T + 2)
+            when_live(divide, n - 1, 0)
             when_live(weighted_values, n - 1, 1)
-            when_live(project, n + 1, 0 if n == 0 else 1)
 
             when_live(exponential, n, 3)
-            if n == 0:
-                round_values(1, 0)
-                project(1, 1)
+            when_first_head(group_features, n + 4, 0)
+            when_first_head(group_features, n + 3, 1)
             when_live(tanh_gate, n - 1, 1)
+            when_live(transpose_e, n, 1)
+            when_live(transpose_qk, n + 2)
             when_live(logits, *divmod(T + 3, NT))
-            when_live(finish, n - 1, 0)
-            when_live(store, n - 1, 0)
             when_live(denominators, n)
             when_live(quantise_e, n, 0)
-            when_first_head(quantise_features, n + 2)
+            when_live(invert, n)
+            when_live(quantise_values, n)
+            when_first_head(quantise_features, n + 3, 0)
+            when_first_head(quantise_features, n + 2, 1)
             search(T + 3)
             negated(T + 3)
-            when_live(transpose_qk, n + 2)
+            when_live(divide, n - 1, 1)
+            when_live(store, n - 1, 0)

@@ -23,6 +23,7 @@ SCALE = DH ** -0.5
 MASKED = -(2.0**127)
 
 UNITS = B * H
+LAST = UNITS - 1
 QK_AHEAD = 6
 LOGIT_BANKS = 3
 
@@ -43,6 +44,12 @@ def tile_attention_pa_t_kernel(tc, q, k1, key_values_input, Wv1_words, Wv1_scale
         turned = stack.enter_context(tc.psum_pool(name="turned", bufs=1))
         side = stack.enter_context(tc.psum_pool(name="side", bufs=2))
         sums = stack.enter_context(tc.psum_pool(name="sums", bufs=2))
+
+        idle = const.tile([P, P * PACK], BF16, align_bytes=64)
+        idle_codes = const.tile([P, P], U32, align_bytes=64)
+        idle_scales = const.tile([P, P], U8, align_bytes=64)
+        nc.vector.memset(idle[:], 0.0)
+        nc.vector.quantize_mx(out=idle_codes[:].bitcast(FP8X4), scales=idle_scales[:], in_=idle[:])
 
         warm = const.tile([P, 1], F32)
         nc.vector.memset(warm[:], 0.0)
@@ -95,36 +102,32 @@ def tile_attention_pa_t_kernel(tc, q, k1, key_values_input, Wv1_words, Wv1_scale
             nc.sync.dma_start(out=k_sb[:], in_=k1[b, h].rearrange("(t p) d -> p t d", p=P))
             kept[unit, "q_sb"], kept[unit, "k_sb"] = q_sb, k_sb
 
-        def transpose_features(b, half):
+        def transpose_features(b, t):
             kv_words = kept[b, "kv_sb"][:].bitcast(F32)
-            kvT_ps = side.tile([P, 2, 2, P], F32, tag="bank")
-            for t2 in range(2):
-                for u in range(2):
-                    nc.tensor.transpose(
-                        kvT_ps[:, t2, u, :], kv_words[:, 2 * half + t2, u : DKV // 2 : 2], ident_f32[:]
-                    )
-            kept[b, "kvT_ps", half] = kvT_ps
+            kvT_ps = (sums if b == 0 else side).tile([P, 2, P], F32, tag="bank")
+            for u in range(2):
+                nc.tensor.transpose(kvT_ps[:, u, :], kv_words[:, t, u : DKV // 2 : 2], ident_f32[:])
+            kept[b, "kvT_ps", t] = kvT_ps
 
-        def group_features(b, half):
-            if half == 0:
+        def group_features(b, t):
+            if t == 0:
                 kv_grouped = loads.tile([P, N * PACK], BF16, align_bytes=64)
                 kept[b, "kv_grouped"] = kv_grouped
             kv_grouped_words = kept[b, "kv_grouped"][:].bitcast(F32).rearrange("p (t j u) -> p t j u", t=NT, u=2)
             nc.scalar.copy(
-                out=kv_grouped_words[:, 2 * half : 2 * half + 2],
-                in_=kept[b, "kvT_ps", half][:].rearrange("p t u j -> p t j u"),
+                out=kv_grouped_words[:, t], in_=kept[b, "kvT_ps", t][:].rearrange("p u j -> p j u")
             )
 
-        def quantise_features(b, half):
-            if half == 0:
+        def quantise_features(b, t):
+            if t == 0:
                 kv_codes = values.tile([P, N], U32, align_bytes=64)
                 kv_scales = values.tile([P, N], U8, align_bytes=64)
                 kept[b, "kv_codes"], kept[b, "kv_scales"] = kv_codes, kv_scales
-            keys = slice(half * 2 * P, (half + 1) * 2 * P)
+            keys = slice(t * P, (t + 1) * P)
             nc.vector.quantize_mx(
                 out=kept[b, "kv_codes"][:, keys].bitcast(FP8X4),
                 scales=kept[b, "kv_scales"][:, keys],
-                in_=kept[b, "kv_grouped"][:, half * 2 * P * PACK : (half + 1) * 2 * P * PACK],
+                in_=kept[b, "kv_grouped"][:, t * P * PACK : (t + 1) * P * PACK],
             )
 
         def project(unit, piece):
@@ -243,44 +246,44 @@ def tile_attention_pa_t_kernel(tc, q, k1, key_values_input, Wv1_words, Wv1_scale
             nc.vector.reciprocal(out=half_inv_den[:], in_=kept[unit, "twice_den"][:])
             kept[unit, "half_inv_den"] = half_inv_den
 
-        def transpose_e(unit, half):
+        def transpose_e(unit, first, count=2):
             e_words = kept[unit, "e_sb"][:].bitcast(F32)
-            eT_ps = turned.tile([P, 2, 2, P], F32, tag="bank")
-            for t2 in range(2):
+            eT_ps = turned.tile([P, count, 2, P], F32, tag="bank")
+            for i in range(count):
                 for u in range(2):
                     nc.tensor.transpose(
-                        eT_ps[:, t2, u, :], e_words[:, 2 * half + t2, u * P : (u + 1) * P], ident_f32[:]
+                        eT_ps[:, i, u, :], e_words[:, first + i, u * P : (u + 1) * P], ident_f32[:]
                     )
-            kept[unit, "eT_ps", half] = eT_ps
+            kept[unit, "eT_ps", first] = eT_ps
 
-        def group_e(unit, half):
-            if half == 0:
+        def group_e(unit, first, count=2):
+            if first == 0:
                 e_grouped = work.tile([P, N * PACK], BF16, align_bytes=64)
                 kept[unit, "e_grouped"] = e_grouped
             e_grouped_words = kept[unit, "e_grouped"][:].bitcast(F32).rearrange("p (t i u) -> p t i u", t=NT, u=2)
             nc.scalar.copy(
-                out=e_grouped_words[:, 2 * half : 2 * half + 2],
-                in_=kept[unit, "eT_ps", half][:].rearrange("p t u i -> p t i u"),
+                out=e_grouped_words[:, first : first + count],
+                in_=kept[unit, "eT_ps", first][:].rearrange("p t u i -> p t i u"),
             )
 
-        def quantise_e(unit, half):
-            if half == 0:
+        def quantise_e(unit, first, count=2):
+            if first == 0:
                 e_codes = work.tile([P, N], U32, align_bytes=64)
                 e_scales = work.tile([P, N], U8, align_bytes=64)
                 kept[unit, "e_codes"], kept[unit, "e_scales"] = e_codes, e_scales
-            queries = slice(half * 2 * P, (half + 1) * 2 * P)
+            queries = slice(first * P, (first + count) * P)
             nc.vector.quantize_mx(
                 out=kept[unit, "e_codes"][:, queries].bitcast(FP8X4),
                 scales=kept[unit, "e_scales"][:, queries],
-                in_=kept[unit, "e_grouped"][:, half * 2 * P * PACK : (half + 1) * 2 * P * PACK],
+                in_=kept[unit, "e_grouped"][:, first * P * PACK : (first + count) * P * PACK],
             )
 
-        def weighted_values(unit, half):
-            acc = sums.tile([P, 2, DV], F32, tag="bank")
-            for t2 in range(2):
-                rows = slice((2 * half + t2) * P, (2 * half + t2 + 1) * P)
+        def weighted_values(unit, first, count=2):
+            acc = (side if unit == LAST else sums).tile([P, count, DV], F32, tag="bank")
+            for i in range(count):
+                rows = slice((first + i) * P, (first + i + 1) * P)
                 nc.tensor.matmul_mx(
-                    out=acc[:, t2, :],
+                    out=acc[:, i, :],
                     lhsT=kept[unit, "e_codes"][:, rows].bitcast(FP8X4),
                     lhsT_scale=kept[unit, "e_scales"][:, rows],
                     rhs=kept[unit, "v_codes"][:].bitcast(FP8X4),
@@ -288,28 +291,25 @@ def tile_attention_pa_t_kernel(tc, q, k1, key_values_input, Wv1_words, Wv1_scale
                     start=True,
                     stop=True,
                 )
-            kept[unit, "acc", half] = acc
-            if half == 0:
-                o_sb = results.tile([P, NT, DV], F32)
-                kept[unit, "o_sb"] = o_sb
+            kept[unit, "acc", first] = acc
 
-        def tanh_gate(unit, half):
-            if half == 0:
+        def half_tanh(unit, first, count=2):
+            if first == 0:
                 tanh_sb = results.tile([P, NT, DV], F32)
                 blend = results.tile([P, NT, DV], F32)
-                kept[unit, "tanh_sb"], kept[unit, "blend"] = tanh_sb, blend
-            for t2 in range(2):
-                it = 2 * half + t2
+                o_sb = results.tile([P, NT, DV], F32)
+                kept[unit, "tanh_sb"], kept[unit, "blend"], kept[unit, "o_sb"] = tanh_sb, blend, o_sb
+            for i in range(count):
                 nc.scalar.activation(
-                    out=kept[unit, "tanh_sb"][:, it, :], in_=kept[unit, "acc", half][:, t2, :], func=FUNC.Tanh,
-                    scale=kept[unit, "half_inv_den"][:, it : it + 1],
+                    out=kept[unit, "tanh_sb"][:, first + i, :], in_=kept[unit, "acc", first][:, i, :], func=FUNC.Tanh,
+                    scale=kept[unit, "half_inv_den"][:, first + i : first + i + 1],
                 )
 
-        def finish(unit, half):
-            pair = slice(2 * half, 2 * half + 2)
+        def finish(unit, first):
+            pair = slice(first, first + 2)
             nc.vector.scalar_tensor_tensor(
                 out=kept[unit, "blend"][:, pair, :], in0=kept[unit, "tanh_sb"][:, pair, :], scalar=1.0,
-                in1=kept[unit, "acc", half][:], op0=ALU.add, op1=ALU.mult,
+                in1=kept[unit, "acc", first][:], op0=ALU.add, op1=ALU.mult,
             )
 
         def divide(unit, it):
@@ -318,20 +318,35 @@ def tile_attention_pa_t_kernel(tc, q, k1, key_values_input, Wv1_words, Wv1_scale
                 scalar1=kept[unit, "half_inv_den"][:, it : it + 1], scalar2=0.0, op0=ALU.mult, op1=ALU.add,
             )
 
-        def store(unit, half):
+        def divide_first(unit, first, count=2):
+            for i in range(count):
+                nc.vector.tensor_scalar(
+                    out=kept[unit, "blend"][:, first + i, :], in0=kept[unit, "acc", first][:, i, :],
+                    scalar1=kept[unit, "half_inv_den"][:, first + i : first + i + 1], scalar2=None, op0=ALU.mult,
+                )
+
+        def finish_last(unit, first, count=2):
+            tiles = slice(first, first + count)
+            nc.vector.scalar_tensor_tensor(
+                out=kept[unit, "o_sb"][:, tiles, :], in0=kept[unit, "tanh_sb"][:, tiles, :], scalar=1.0,
+                in1=kept[unit, "blend"][:, tiles, :], op0=ALU.add, op1=ALU.mult,
+            )
+
+        def store(unit, first, count=2):
             b, h = divmod(unit, H)
             nc.sync.dma_start(
-                out=out[b, h, half * 2 * P : (half + 1) * 2 * P, :].rearrange("(t p) c -> p t c", p=P),
-                in_=kept[unit, "o_sb"][:, 2 * half : 2 * half + 2, :],
+                out=out[b, h, first * P : (first + count) * P, :].rearrange("(t p) c -> p t c", p=P),
+                in_=kept[unit, "o_sb"][:, first : first + count, :],
             )
 
         def when_live(stage, unit, *args):
             if 0 <= unit < UNITS:
                 stage(unit, *args)
 
-        def when_first_head(stage, unit, *args):
-            if 0 <= unit < UNITS and unit % H == 0:
-                stage(unit // H, *args)
+        def next_sequence(stage, n):
+            b, t = divmod(n, H)
+            if b + 1 < B:
+                stage(b + 1, t)
 
         def search(tile):
             when_live(maximum, *divmod(tile, NT))
@@ -359,35 +374,54 @@ def tile_attention_pa_t_kernel(tc, q, k1, key_values_input, Wv1_words, Wv1_scale
         load_qk(3)
 
         stack.enter_context(tc.manual_schedule())
+        def warm_up(passes):
+            bank = logit_banks.tile([P, P], F32, tag="bank")
+            for i in range(passes):
+                nc.tensor.matmul_mx(
+                    out=bank[:], lhsT=idle_codes[:].bitcast(FP8X4), lhsT_scale=idle_scales[:],
+                    rhs=idle_codes[:].bitcast(FP8X4), rhs_scale=idle_scales[:], start=True, stop=True,
+                )
+        warm_up(12)
         transpose_qk(0)
-        copy_qk(0)
-        transpose_features(0, 0)
-        group_features(0, 0)
+        warm_up(8)
+        qkT = work.tile([P, 2 * N], BF16)
+        nc.scalar.copy(out=qkT[:, 0:N], in_=kept[0, "qkT_ps"][:, 0:NT, :].rearrange("p t i -> p (t i)"))
+        nc.vector.tensor_copy(out=qkT[:, N:], in_=kept[0, "qkT_ps"][:, NT:, :].rearrange("p t i -> p (t i)"))
+        kept[0, "qkT"] = qkT
         logits(0, 0)
         maximum(0, 0)
         negate(0, 0)
+        transpose_features(0, 0)
+        transpose_features(0, 1)
+        group_features(0, 0)
+        group_features(0, 1)
         logits(0, 1)
         maximum(0, 1)
         negate(0, 1)
-        transpose_features(0, 1)
-        group_features(0, 1)
-        transpose_qk(1)
-        quantise_features(0, 0)
+        transpose_features(0, 2)
+        transpose_features(0, 3)
         logits(0, 2)
         maximum(0, 2)
         negate(0, 2)
+        quantise_features(0, 0)
         quantise_features(0, 1)
-        for n in range(UNITS + 2):
+        transpose_qk(1)
+        for n in range(UNITS):
             when_live(load_qk, n + 4)
             if n % H == 0 and n // H + 2 < B:
                 load_features(n // H + 2)
             T = n * NT + LOGIT_BANKS
 
             when_live(exponential, n, 0)
+            if n == 0:
+                group_features(0, 2)
+                group_features(0, 3)
+                quantise_features(0, 2)
+                quantise_features(0, 3)
             when_live(copy_qk, n + 1)
-            when_live(group_e, n - 1, 1)
+            when_live(group_e, n - 1, 2)
             when_live(logits, *divmod(T, NT))
-            when_live(finish, n - 2, 1)
+            when_live(finish, n - 2, 2)
             search(T)
             negated(T)
             when_live(divide, n - 2, 2)
@@ -395,43 +429,65 @@ def tile_attention_pa_t_kernel(tc, q, k1, key_values_input, Wv1_words, Wv1_scale
             when_live(project, n, 0)
 
             when_live(exponential, n, 1)
-            when_live(tanh_gate, n - 1, 0)
+            when_live(half_tanh, n - 1, 0)
             when_live(transpose_e, n, 0)
             when_live(logits, *divmod(T + 1, NT))
+            when_live(quantise_e, n - 1, 2)
             when_live(round_values, n, 0)
-            when_live(quantise_e, n - 1, 1)
             search(T + 1)
             negated(T + 1)
             when_live(divide, n - 2, 3)
-            when_live(store, n - 2, 1)
+            when_live(store, n - 2, 2)
             when_live(project, n, 1)
+            when_live(weighted_values, n - 1, 2)
 
             when_live(exponential, n, 2)
             when_live(group_e, n, 0)
-            when_first_head(transpose_features, n + 4, 0)
-            when_first_head(transpose_features, n + 3, 1)
+            next_sequence(transpose_features, n)
             when_live(logits, *divmod(T + 2, NT))
             when_live(finish, n - 1, 0)
             when_live(round_values, n, 1)
             search(T + 2)
             negated(T + 2)
             when_live(divide, n - 1, 0)
-            when_live(weighted_values, n - 1, 1)
 
             when_live(exponential, n, 3)
-            when_first_head(group_features, n + 4, 0)
-            when_first_head(group_features, n + 3, 1)
-            when_live(tanh_gate, n - 1, 1)
-            when_live(transpose_e, n, 1)
+            next_sequence(group_features, n)
+            when_live(half_tanh, n - 1, 2)
+            when_live(transpose_e, n, 2, 1 if n == LAST else 2)
             when_live(transpose_qk, n + 2)
             when_live(logits, *divmod(T + 3, NT))
             when_live(denominators, n)
             when_live(quantise_e, n, 0)
             when_live(invert, n)
             when_live(quantise_values, n)
-            when_first_head(quantise_features, n + 3, 0)
-            when_first_head(quantise_features, n + 2, 1)
+            next_sequence(quantise_features, n)
             search(T + 3)
             negated(T + 3)
             when_live(divide, n - 1, 1)
             when_live(store, n - 1, 0)
+
+        group_e(LAST, 2, 1)
+        transpose_e(LAST, 3, 1)
+        weighted_values(LAST, 0)
+        group_e(LAST, 3, 1)
+        finish(LAST - 1, 2)
+        quantise_e(LAST, 2, 1)
+        weighted_values(LAST, 2, 1)
+        quantise_e(LAST, 3, 1)
+        half_tanh(LAST, 0)
+        divide_first(LAST, 0)
+        for it in (2, 3):
+            divide(LAST - 1, it)
+        store(LAST - 1, 2)
+        finish_last(LAST, 0)
+        store(LAST, 0)
+        half_tanh(LAST, 2, 1)
+        divide_first(LAST, 2, 1)
+        weighted_values(LAST, 3, 1)
+        finish_last(LAST, 2, 1)
+        store(LAST, 2, 1)
+        half_tanh(LAST, 3, 1)
+        divide_first(LAST, 3, 1)
+        finish_last(LAST, 3, 1)
+        store(LAST, 3, 1)

@@ -20,6 +20,7 @@ P = 128
 NT = N // P
 PACK = 4
 SCALE = DH ** -0.5
+PLAIN_MASKS = (0, 2, 2, 0)
 MASKED = -(2.0**127)
 
 UNITS = B * H
@@ -64,20 +65,28 @@ def tile_attention_pa_t_kernel(tc, q, k1, key_values_input, Wv1_words, Wv1_scale
         ident_bf = const.tile([P, P], BF16)
         make_identity(nc, ident_bf[:])
 
-        mask_f32 = const.tile([P, P], F32)
-        nc.gpsimd.memset(mask_f32[:], 0.0)
+        mask_T = const.tile([P, 2, P], F32)
+        nc.gpsimd.memset(mask_T[:], 0.0)
         nc.gpsimd.affine_select(
-            out=mask_f32[:], in_=mask_f32[:], pattern=[[-1, P]], compare_op=ALU.is_ge,
-            fill=MASKED, base=0, channel_multiplier=1,
+            out=mask_T[:, 0, :], in_=mask_T[:, 0, :], pattern=[[1, P]], compare_op=ALU.is_ge,
+            fill=MASKED, base=0, channel_multiplier=-1,
         )
-        mask_own = const.tile([P, P], BF16)
-        nc.vector.tensor_copy(out=mask_own[:], in_=mask_f32[:])
-        mask_next_T = const.tile([P, P], F32)
-        nc.gpsimd.memset(mask_next_T[:], 0.0)
         nc.gpsimd.affine_select(
-            out=mask_next_T[:], in_=mask_next_T[:], pattern=[[-1, P]], compare_op=ALU.is_ge,
+            out=mask_T[:, 1, :], in_=mask_T[:, 1, :], pattern=[[-1, P]], compare_op=ALU.is_ge,
             fill=MASKED, base=-1, channel_multiplier=1,
         )
+        mask_f32 = const.tile([P, 2, P], F32)
+        nc.gpsimd.memset(mask_f32[:], 0.0)
+        nc.gpsimd.affine_select(
+            out=mask_f32[:, 0, :], in_=mask_f32[:, 0, :], pattern=[[-1, P]], compare_op=ALU.is_ge,
+            fill=MASKED, base=0, channel_multiplier=1,
+        )
+        nc.gpsimd.affine_select(
+            out=mask_f32[:, 1, :], in_=mask_f32[:, 1, :], pattern=[[1, P]], compare_op=ALU.is_ge,
+            fill=MASKED, base=-1, channel_multiplier=-1,
+        )
+        mask = const.tile([P, 2, P], BF16)
+        nc.vector.tensor_copy(out=mask[:], in_=mask_f32[:])
 
         sink_bf = const.tile([P, H], BF16)
         sink = const.tile([P, H], F32)
@@ -187,13 +196,17 @@ def tile_attention_pa_t_kernel(tc, q, k1, key_values_input, Wv1_words, Wv1_scale
                 start=True,
                 stop=False,
             )
-            nc.tensor.matmul(
-                out=s_ps[:, it, :], lhsT=ident_bf[:], rhs=mask_own[:], start=False, stop=(it == NT - 1)
-            )
-            if it < NT - 1:
+            plain = PLAIN_MASKS[it]
+            masked = min(2, NT - it)
+            if plain > 0:
                 nc.tensor.matmul(
-                    out=s_ps[:, it + 1, :], lhsT=mask_next_T[:], rhs=ident_f32[:], is_transpose=True,
-                    start=False, stop=True,
+                    out=s_ps[:, it : it + plain, :].rearrange("p a j -> p (a j)"), lhsT=ident_bf[:],
+                    rhs=mask[:, 0:plain, :].rearrange("p a j -> p (a j)"), start=False, stop=(plain == masked),
+                )
+            for a in range(plain, masked):
+                nc.tensor.matmul(
+                    out=s_ps[:, it + a, :], lhsT=mask_T[:, a, :], rhs=ident_f32[:], is_transpose=True,
+                    start=False, stop=(a == masked - 1),
                 )
             kept[unit, "s_ps", it] = s_ps
 

import math
from contextlib import ExitStack

import concourse.mybir as mybir
from concourse.masks import make_identity

F32 = mybir.dt.float32
BF16 = mybir.dt.bfloat16
I32 = mybir.dt.int32
U32 = mybir.dt.uint32
U8 = mybir.dt.uint8
FP8X4 = mybir.dt.float8_e4m3fn_x4
ALU = mybir.AluOpType
FUNC = mybir.ActivationFunctionType
AXIS = mybir.AxisListType

B, H, N, DH, DV, DKV = 8, 4, 512, 128, 256, 512
DM = H * DV
P = 128
NT = N // P
PACK = 4
SCALE = DH ** -0.5
PLAIN_MASKS = (0, 2, 2, 0)
MASKED = -(2.0**127)

UNITS = B * H
LAST = UNITS - 1
QK_AHEAD = 6
LOGIT_BANKS = 3

FLOPS = 2 * B * N * DKV * DM + 2 * B * H * N * N * DH + 2 * B * H * N * N * DV


def tile_attention_pa_t_kernel(tc, q, k1, key_values_input, Wv1_words, Wv1_scales, attn_sink, out):
    nc = tc.nc
    with ExitStack() as stack:
        const = stack.enter_context(tc.tile_pool(name="const", bufs=1))
        loads = stack.enter_context(tc.tile_pool(name="loads", bufs=3))
        unit_loads = stack.enter_context(tc.tile_pool(name="unit_loads", bufs=QK_AHEAD + 1))
        values = stack.enter_context(tc.tile_pool(name="values", bufs=4))
        work = stack.enter_context(tc.tile_pool(name="work", bufs=3))
        results = stack.enter_context(tc.tile_pool(name="results", bufs=3))
        small = stack.enter_context(tc.tile_pool(name="small", bufs=4))
        logit_banks = stack.enter_context(tc.psum_pool(name="logit_banks", bufs=LOGIT_BANKS))
        turned = stack.enter_context(tc.psum_pool(name="turned", bufs=1))
        side = stack.enter_context(tc.psum_pool(name="side", bufs=2))
        sums = stack.enter_context(tc.psum_pool(name="sums", bufs=2))

        idle = const.tile([P, P * PACK], BF16, align_bytes=64)
        idle_codes = const.tile([P, P], U32, align_bytes=64)
        idle_scales = const.tile([P, P], U8, align_bytes=64)
        nc.vector.memset(idle[:], 0.0)
        nc.vector.quantize_mx(out=idle_codes[:].bitcast(FP8X4), scales=idle_scales[:], in_=idle[:])

        warm = const.tile([P, 1], F32)
        nc.vector.memset(warm[:], 0.0)
        nc.scalar.activation(out=warm[:], in_=warm[:], func=FUNC.Exp)

        w_codes = const.tile([P, DM], U32, align_bytes=64)
        w_scales = const.tile([P, DM], U8, align_bytes=64)
        nc.vector.memset(w_scales[:].bitcast(I32), 0)

        ident_f32 = const.tile([P, P], F32)
        make_identity(nc, ident_f32[:])
        ident_bf = const.tile([P, P], BF16)
        make_identity(nc, ident_bf[:])

        mask_T = const.tile([P, 2, P], F32)
        nc.gpsimd.memset(mask_T[:], 0.0)
        nc.gpsimd.affine_select(
            out=mask_T[:, 0, :], in_=mask_T[:, 0, :], pattern=[[1, P]], compare_op=ALU.is_ge,
            fill=MASKED, base=0, channel_multiplier=-1,
        )
        nc.gpsimd.affine_select(
            out=mask_T[:, 1, :], in_=mask_T[:, 1, :], pattern=[[-1, P]], compare_op=ALU.is_ge,
            fill=MASKED, base=-1, channel_multiplier=1,
        )
        mask_f32 = const.tile([P, 2, P], F32)
        nc.gpsimd.memset(mask_f32[:], 0.0)
        nc.gpsimd.affine_select(
            out=mask_f32[:, 0, :], in_=mask_f32[:, 0, :], pattern=[[-1, P]], compare_op=ALU.is_ge,
            fill=MASKED, base=0, channel_multiplier=1,
        )
        nc.gpsimd.affine_select(
            out=mask_f32[:, 1, :], in_=mask_f32[:, 1, :], pattern=[[1, P]], compare_op=ALU.is_ge,
            fill=MASKED, base=-1, channel_multiplier=-1,
        )
        mask = const.tile([P, 2, P], BF16)
        nc.vector.tensor_copy(out=mask[:], in_=mask_f32[:])

        sink_bf = const.tile([P, H], BF16)
        sink = const.tile([P, H], F32)
        neg_sink = const.tile([P, H], F32)
        sink_ln2 = const.tile([P, H], F32)

        kept = {}

        def load_features(b):
            kv_sb = loads.tile([P, NT, DKV], BF16)
            nc.sync.dma_start(
                out=kv_sb[:].rearrange("p (u e) k -> p u (e k)", e=2),
                in_=key_values_input[b].rearrange("(u p e) k -> p u (e k)", u=2, e=2),
            )
            kept[b, "kv_sb"] = kv_sb

        def load_qk(unit):
            b, h = divmod(unit, H)
            q_sb = unit_loads.tile([P, NT, DH], BF16)
            nc.sync.dma_start(out=q_sb[:], in_=q[b, h].rearrange("(t p) d -> p t d", p=P))
            k_sb = unit_loads.tile([P, NT, DH], BF16)
            nc.sync.dma_start(out=k_sb[:], in_=k1[b, h].rearrange("(t p) d -> p t d", p=P))
            kept[unit, "q_sb"], kept[unit, "k_sb"] = q_sb, k_sb

        def transpose_features(b, t):
            kv_words = kept[b, "kv_sb"][:].bitcast(F32)
            kvT_ps = (sums if b == 0 else side).tile([P, 2, P], F32, tag="bank")
            for u in range(2):
                nc.tensor.transpose(kvT_ps[:, u, :], kv_words[:, t, u : DKV // 2 : 2], ident_f32[:])
            kept[b, "kvT_ps", t] = kvT_ps

        def group_features(b, t):
            if t == 0:
                kv_grouped = loads.tile([P, N * PACK], BF16, align_bytes=64)
                kept[b, "kv_grouped"] = kv_grouped
            kv_grouped_words = kept[b, "kv_grouped"][:].bitcast(F32).rearrange("p (t j u) -> p t j u", t=NT, u=2)
            nc.scalar.copy(
                out=kv_grouped_words[:, t], in_=kept[b, "kvT_ps", t][:].rearrange("p u j -> p j u")
            )

        def quantise_features(b, t):
            if t == 0:
                kv_codes = values.tile([P, N], U32, align_bytes=64)
                kv_scales = values.tile([P, N], U8, align_bytes=64)
                kept[b, "kv_codes"], kept[b, "kv_scales"] = kv_codes, kv_scales
            keys = slice(t * P, (t + 1) * P)
            nc.vector.quantize_mx(
                out=kept[b, "kv_codes"][:, keys].bitcast(FP8X4),
                scales=kept[b, "kv_scales"][:, keys],
                in_=kept[b, "kv_grouped"][:, t * P * PACK : (t + 1) * P * PACK],
            )

        def project(unit, piece):
            b, h = divmod(unit, H)
            cols = slice((2 * h + piece) * P, (2 * h + piece + 1) * P)
            v_ps = side.tile([P, NT, P], F32, tag="bank")
            for t in range(NT):
                rows = slice(t * P, (t + 1) * P)
                nc.tensor.matmul_mx(
                    out=v_ps[:, t, :],
                    lhsT=kept[b, "kv_codes"][:, rows].bitcast(FP8X4),
                    lhsT_scale=kept[b, "kv_scales"][:, rows],
                    rhs=w_codes[:, cols].bitcast(FP8X4),
                    rhs_scale=w_scales[:, cols],
                    start=True,
                    stop=True,
                )
            kept[unit, "v_ps", piece] = v_ps

        def round_values(unit, piece):
            if piece == 0:
                v_grouped = work.tile([P, DV * PACK], BF16, align_bytes=64)
                kept[unit, "v_grouped"] = v_grouped
            first = piece * P * PACK
            grouped = kept[unit, "v_grouped"][:, first : first + P * PACK].rearrange("p (n t) -> p n t", t=PACK)
            by_column = kept[unit, "v_ps", piece][:].rearrange("p t n -> p n t")
            nc.vector.tensor_copy(out=grouped, in_=by_column)

        def quantise_values(unit):
            v_codes = values.tile([P, DV], U32, align_bytes=64)
            v_scales = values.tile([P, DV], U8, align_bytes=64)
            kept[unit, "v_codes"], kept[unit, "v_scales"] = v_codes, v_scales
            nc.vector.quantize_mx(
                out=v_codes[:].bitcast(FP8X4), scales=v_scales[:], in_=kept[unit, "v_grouped"][:]
            )

        def transpose_qk(unit):
            qkT_ps = side.tile([P, 2 * NT, P], BF16, tag="bank")
            for t in range(NT):
                nc.tensor.transpose(qkT_ps[:, t, :], kept[unit, "q_sb"][:, t, :], ident_bf[:])
            for t in range(NT):
                nc.tensor.transpose(qkT_ps[:, NT + t, :], kept[unit, "k_sb"][:, t, :], ident_bf[:])
            kept[unit, "qkT_ps"] = qkT_ps

        def copy_qk(unit):
            qkT = work.tile([P, 2 * N], BF16)
            nc.scalar.copy(out=qkT[:], in_=kept[unit, "qkT_ps"][:].rearrange("p t i -> p (t i)"))
            kept[unit, "qkT"] = qkT

        def logits(unit, it):
            qkT = kept[unit, "qkT"]
            s_ps = logit_banks.tile([P, NT, P], F32, tag="bank")
            nc.tensor.matmul(
                out=s_ps[:].rearrange("p a j -> p (a j)"),
                lhsT=qkT[:, it * P : (it + 1) * P],
                rhs=qkT[:, N : 2 * N],
                start=True,
                stop=False,
            )
            plain = PLAIN_MASKS[it]
            masked = min(2, NT - it)
            if plain > 0:
                nc.tensor.matmul(
                    out=s_ps[:, it : it + plain, :].rearrange("p a j -> p (a j)"), lhsT=ident_bf[:],
                    rhs=mask[:, 0:plain, :].rearrange("p a j -> p (a j)"), start=False, stop=(plain == masked),
                )
            for a in range(plain, masked):
                nc.tensor.matmul(
                    out=s_ps[:, it + a, :], lhsT=mask_T[:, a, :], rhs=ident_f32[:], is_transpose=True,
                    start=False, stop=(a == masked - 1),
                )
            kept[unit, "s_ps", it] = s_ps

        def maximum(unit, it):
            if it == 0:
                s_max = small.tile([P, NT], F32)
                neg_m = small.tile([P, NT], F32)
                kept[unit, "s_max"], kept[unit, "neg_m"] = s_max, neg_m
            column = slice(it, it + 1)
            nc.vector.tensor_reduce(
                out=kept[unit, "s_max"][:, column], in_=kept[unit, "s_ps", it][:], axis=AXIS.XY, op=ALU.max
            )

        def negate(unit, it):
            h = unit % H
            column = slice(it, it + 1)
            nc.gpsimd.tensor_scalar(
                out=kept[unit, "neg_m"][:, column], in0=kept[unit, "s_max"][:, column], scalar1=-SCALE,
                scalar2=neg_sink[:, h : h + 1], op0=ALU.mult, op1=ALU.min,
            )

        def exponential(unit, it):
            h = unit % H
            neg_m = kept[unit, "neg_m"]
            if it == 0:
                e_sb = work.tile([P, NT, N], BF16)
                den_parts = small.tile([P, NT, 2], F32)
                kept[unit, "e_sb"], kept[unit, "den_parts"] = e_sb, den_parts
            e_sb, den_parts = kept[unit, "e_sb"], kept[unit, "den_parts"]
            nc.scalar.activation(
                out=e_sb[:, it, :], in_=kept[unit, "s_ps", it][:].rearrange("p a j -> p (a j)"), func=FUNC.Exp,
                bias=neg_m[:, it : it + 1], scale=SCALE, accum_out=den_parts[:, it, 0:1],
            )
            if it == NT - 1:
                nc.scalar.activation(
                    out=den_parts[:, :, 1], in_=neg_m[:], func=FUNC.Exp, bias=sink_ln2[:, h : h + 1], scale=1.0
                )

        def denominators(unit):
            den_parts = kept[unit, "den_parts"]
            twice_den = small.tile([P, NT], F32)
            nc.vector.scalar_tensor_tensor(
                out=twice_den[:], in0=den_parts[:, :, 0], scalar=2.0, in1=den_parts[:, :, 1],
                op0=ALU.mult, op1=ALU.add,
            )
            kept[unit, "twice_den"] = twice_den

        def invert(unit):
            half_inv_den = small.tile([P, NT], F32)
            nc.vector.reciprocal(out=half_inv_den[:], in_=kept[unit, "twice_den"][:])
            kept[unit, "half_inv_den"] = half_inv_den

        def transpose_e(unit, first, count=2):
            e_words = kept[unit, "e_sb"][:].bitcast(F32)
            eT_ps = turned.tile([P, count, 2, P], F32, tag="bank")
            for i in range(count):
                for u in range(2):
                    nc.tensor.transpose(
                        eT_ps[:, i, u, :], e_words[:, first + i, u * P : (u + 1) * P], ident_f32[:]
                    )
            kept[unit, "eT_ps", first] = eT_ps

        def group_e(unit, first, count=2):
            if first == 0:
                e_grouped = work.tile([P, N * PACK], BF16, align_bytes=64)
                kept[unit, "e_grouped"] = e_grouped
            e_grouped_words = kept[unit, "e_grouped"][:].bitcast(F32).rearrange("p (t i u) -> p t i u", t=NT, u=2)
            nc.scalar.copy(
                out=e_grouped_words[:, first : first + count],
                in_=kept[unit, "eT_ps", first][:].rearrange("p t u i -> p t i u"),
            )

        def quantise_e(unit, first, count=2):
            if first == 0:
                e_codes = work.tile([P, N], U32, align_bytes=64)
                e_scales = work.tile([P, N], U8, align_bytes=64)
                kept[unit, "e_codes"], kept[unit, "e_scales"] = e_codes, e_scales
            queries = slice(first * P, (first + count) * P)
            nc.vector.quantize_mx(
                out=kept[unit, "e_codes"][:, queries].bitcast(FP8X4),
                scales=kept[unit, "e_scales"][:, queries],
                in_=kept[unit, "e_grouped"][:, first * P * PACK : (first + count) * P * PACK],
            )

        def weighted_values(unit, first, count=2):
            acc = (side if unit == LAST else sums).tile([P, count, DV], F32, tag="bank")
            for i in range(count):
                rows = slice((first + i) * P, (first + i + 1) * P)
                nc.tensor.matmul_mx(
                    out=acc[:, i, :],
                    lhsT=kept[unit, "e_codes"][:, rows].bitcast(FP8X4),
                    lhsT_scale=kept[unit, "e_scales"][:, rows],
                    rhs=kept[unit, "v_codes"][:].bitcast(FP8X4),
                    rhs_scale=kept[unit, "v_scales"][:],
                    start=True,
                    stop=True,
                )
            kept[unit, "acc", first] = acc

        def half_tanh(unit, first, count=2):
            if first == 0:
                tanh_sb = results.tile([P, NT, DV], F32)
                blend = results.tile([P, NT, DV], F32)
                o_sb = results.tile([P, NT, DV], F32)
                kept[unit, "tanh_sb"], kept[unit, "blend"], kept[unit, "o_sb"] = tanh_sb, blend, o_sb
            for i in range(count):
                nc.scalar.activation(
                    out=kept[unit, "tanh_sb"][:, first + i, :], in_=kept[unit, "acc", first][:, i, :], func=FUNC.Tanh,
                    scale=kept[unit, "half_inv_den"][:, first + i : first + i + 1],
                )

        def finish(unit, first):
            pair = slice(first, first + 2)
            nc.vector.scalar_tensor_tensor(
                out=kept[unit, "blend"][:, pair, :], in0=kept[unit, "tanh_sb"][:, pair, :], scalar=1.0,
                in1=kept[unit, "acc", first][:], op0=ALU.add, op1=ALU.mult,
            )

        def divide(unit, it):
            nc.gpsimd.tensor_scalar(
                out=kept[unit, "o_sb"][:, it, :], in0=kept[unit, "blend"][:, it, :],
                scalar1=kept[unit, "half_inv_den"][:, it : it + 1], scalar2=0.0, op0=ALU.mult, op1=ALU.add,
            )

        def divide_first(unit, first, count=2):
            for i in range(count):
                nc.vector.tensor_scalar(
                    out=kept[unit, "blend"][:, first + i, :], in0=kept[unit, "acc", first][:, i, :],
                    scalar1=kept[unit, "half_inv_den"][:, first + i : first + i + 1], scalar2=None, op0=ALU.mult,
                )

        def finish_last(unit, first, count=2):
            tiles = slice(first, first + count)
            nc.vector.scalar_tensor_tensor(
                out=kept[unit, "o_sb"][:, tiles, :], in0=kept[unit, "tanh_sb"][:, tiles, :], scalar=1.0,
                in1=kept[unit, "blend"][:, tiles, :], op0=ALU.add, op1=ALU.mult,
            )

        def store(unit, first, count=2):
            b, h = divmod(unit, H)
            nc.sync.dma_start(
                out=out[b, h, first * P : (first + count) * P, :].rearrange("(t p) c -> p t c", p=P),
                in_=kept[unit, "o_sb"][:, first : first + count, :],
            )

        def when_live(stage, unit, *args):
            if 0 <= unit < UNITS:
                stage(unit, *args)

        def next_sequence(stage, n):
            b, t = divmod(n, H)
            if b + 1 < B:
                stage(b + 1, t)

        def search(tile):
            when_live(maximum, *divmod(tile, NT))

        def negated(tile):
            when_live(negate, *divmod(tile, NT))

        load_qk(0)
        load_qk(1)
        nc.sync.dma_start(out=sink_bf[:], in_=attn_sink.partition_broadcast(P))
        nc.vector.tensor_copy(out=sink[:], in_=sink_bf[:])
        nc.vector.tensor_scalar(out=neg_sink[:], in0=sink[:], scalar1=-1.0, scalar2=None, op0=ALU.mult)
        nc.vector.tensor_scalar(out=sink_ln2[:], in0=sink[:], scalar1=math.log(2.0), scalar2=None, op0=ALU.add)
        load_features(0)
        for quad in range(4):
            nc.sync.dma_start(
                out=w_scales[32 * quad : 32 * quad + 4, :].bitcast(I32),
                in_=Wv1_scales[0, 4 * quad : 4 * quad + 4, :].bitcast(I32),
            )
        nc.sync.dma_start(
            out=w_codes[:].bitcast(I32), in_=Wv1_words[0].rearrange("p n t -> p (n t)").bitcast(I32)
        )
        load_qk(2)
        load_features(1)
        load_qk(3)

        stack.enter_context(tc.manual_schedule())
        def warm_up(passes):
            bank = logit_banks.tile([P, P], F32, tag="bank")
            for i in range(passes):
                nc.tensor.matmul_mx(
                    out=bank[:], lhsT=idle_codes[:].bitcast(FP8X4), lhsT_scale=idle_scales[:],
                    rhs=idle_codes[:].bitcast(FP8X4), rhs_scale=idle_scales[:], start=True, stop=True,
                )
        warm_up(12)
        transpose_qk(0)
        warm_up(8)
        qkT = work.tile([P, 2 * N], BF16)
        nc.scalar.copy(out=qkT[:, 0:N], in_=kept[0, "qkT_ps"][:, 0:NT, :].rearrange("p t i -> p (t i)"))
        nc.vector.tensor_copy(out=qkT[:, N:], in_=kept[0, "qkT_ps"][:, NT:, :].rearrange("p t i -> p (t i)"))
        kept[0, "qkT"] = qkT
        logits(0, 0)
        maximum(0, 0)
        negate(0, 0)
        transpose_features(0, 0)
        transpose_features(0, 1)
        group_features(0, 0)
        group_features(0, 1)
        logits(0, 1)
        maximum(0, 1)
        negate(0, 1)
        transpose_features(0, 2)
        transpose_features(0, 3)
        logits(0, 2)
        maximum(0, 2)
        negate(0, 2)
        quantise_features(0, 0)
        quantise_features(0, 1)
        transpose_qk(1)
        for n in range(UNITS):
            when_live(load_qk, n + 4)
            if n % H == 0 and n // H + 2 < B:
                load_features(n // H + 2)
            T = n * NT + LOGIT_BANKS

            when_live(exponential, n, 0)
            if n == 0:
                group_features(0, 2)
                group_features(0, 3)
                quantise_features(0, 2)
                quantise_features(0, 3)
            when_live(copy_qk, n + 1)
            when_live(group_e, n - 1, 2)
            when_live(logits, *divmod(T, NT))
            when_live(finish, n - 2, 2)
            search(T)
            negated(T)
            when_live(divide, n - 2, 2)
            when_live(weighted_values, n - 1, 0)
            when_live(project, n, 0)

            when_live(exponential, n, 1)
            when_live(half_tanh, n - 1, 0)
            when_live(transpose_e, n, 0)
            when_live(logits, *divmod(T + 1, NT))
            when_live(quantise_e, n - 1, 2)
            when_live(round_values, n, 0)
            search(T + 1)
            negated(T + 1)
            when_live(divide, n - 2, 3)
            when_live(store, n - 2, 2)
            when_live(project, n, 1)
            when_live(weighted_values, n - 1, 2)

            when_live(exponential, n, 2)
            when_live(group_e, n, 0)
            next_sequence(transpose_features, n)
            when_live(logits, *divmod(T + 2, NT))
            when_live(finish, n - 1, 0)
            when_live(round_values, n, 1)
            search(T + 2)
            negated(T + 2)
            when_live(divide, n - 1, 0)

            when_live(exponential, n, 3)
            next_sequence(group_features, n)
            when_live(half_tanh, n - 1, 2)
            when_live(transpose_e, n, 2, 1 if n == LAST else 2)
            when_live(transpose_qk, n + 2)
            when_live(logits, *divmod(T + 3, NT))
            when_live(denominators, n)
            when_live(quantise_e, n, 0)
            when_live(invert, n)
            when_live(quantise_values, n)
            next_sequence(quantise_features, n)
            search(T + 3)
            negated(T + 3)
            when_live(divide, n - 1, 1)
            when_live(store, n - 1, 0)

        group_e(LAST, 2, 1)
        transpose_e(LAST, 3, 1)
        weighted_values(LAST, 0)
        group_e(LAST, 3, 1)
        finish(LAST - 1, 2)
        quantise_e(LAST, 2, 1)
        weighted_values(LAST, 2, 1)
        quantise_e(LAST, 3, 1)
        half_tanh(LAST, 0)
        divide_first(LAST, 0)
        for it in (2, 3):
            divide(LAST - 1, it)
        store(LAST - 1, 2)
        finish_last(LAST, 0)
        store(LAST, 0)
        half_tanh(LAST, 2, 1)
        divide_first(LAST, 2, 1)
        weighted_values(LAST, 3, 1)
        finish_last(LAST, 2, 1)
        store(LAST, 2, 1)
        half_tanh(LAST, 3, 1)
        divide_first(LAST, 3, 1)
        finish_last(LAST, 3, 1)
        store(LAST, 3, 1)
